import numpy as np
import ml_dtypes


def mxq(x, axis, fmt="e4m3"):
    dtype, down = {"e4m3": (ml_dtypes.float8_e4m3fn, 7), "e5m2": (ml_dtypes.float8_e5m2, 14)}[fmt]
    v = np.moveaxis(np.asarray(x, np.float32).astype(ml_dtypes.bfloat16).astype(np.float64), axis, -1)
    blocks = v.reshape(v.shape[:-1] + (-1, 32))
    amax = np.abs(blocks).max(-1, keepdims=True)
    byte = np.maximum(np.where(amax > 0, np.frexp(amax)[1] - 1 + 127, 0) - down, 1)
    scale = np.exp2(byte - 127.0)
    codes = (blocks / scale).astype(np.float32).astype(dtype).astype(np.float64)
    return np.moveaxis((codes * scale).reshape(v.shape), -1, axis)


WIDE = False


def mx_kscale(k):
    if not WIDE:
        return np.ones(k)
    levels = np.array([10, -10, 5, -5, 0])
    a = np.random.permutation(np.resize(levels, k // 512 * 4)).reshape(k // 512, 4)
    idx = np.arange(k)
    return np.exp2(a[idx // 512, idx % 128 // 32])


BF16 = ml_dtypes.bfloat16


def bf(x):
    return np.asarray(x, np.float32).astype(BF16)


def f64(x):
    return np.asarray(x).astype(np.float64)


B, S, E, H, F = 1, 512, 1024, 16, 4096
D = E // H


def setup_inputs():
    t = mx_kscale(E)
    return {
        "q": bf(np.random.standard_normal((B, S, E)) * 0.7),
        "k": bf(np.random.standard_normal((B, S, E)) * 0.7),
        "v": bf(np.random.standard_normal((B, S, E)) * 0.7 * t),
        "x": bf(np.random.standard_normal((B, S, E))),
        "w_proj": bf(np.random.standard_normal((E, E)) * 2.0 / np.sqrt(E) / t[:, None]),
        "b_proj": bf(np.random.standard_normal(E) * 0.1),
    }


def reference(q, k, v, x, w_proj, b_proj):
    scores = f64(q) @ f64(k).transpose(0, 2, 1) / np.sqrt(D)
    e = np.exp(scores - scores.max(-1, keepdims=True))
    attn = (mxq(e, 2, "e4m3") @ mxq(f64(v), 1, "e4m3")) / e.sum(-1, keepdims=True)
    a = (mxq(attn, 2, "e4m3") @ mxq(f64(w_proj), 0, "e4m3")) + f64(b_proj)
    return f64(x) + a

@@ -1,0 +1,317 @@
+from contextlib import ExitStack
+
+import concourse.mybir as mybir
+from concourse.masks import make_identity
+
+F32 = mybir.dt.float32
+BF16 = mybir.dt.bfloat16
+U32 = mybir.dt.uint32
+U8 = mybir.dt.uint8
+FP8X4 = mybir.dt.float8_e4m3fn_x4
+ALU = mybir.AluOpType
+ACT = mybir.ActivationFunctionType
+AXIS = mybir.AxisListType
+
+P = 128
+PACK = 4
+S = 512
+E = 1024
+HEAD = 64
+BANK = 512
+SCORE_SCALE = HEAD**-0.5
+
+Q_TILES = S // P
+E_CHUNKS = E // P
+F_PASSES = E // (P * PACK)
+HALVES = E // BANK
+
+FLOPS = 2 * S * S * E + 2 * S * S * E + 2 * S * E * E
+
+
+def tile_transformerblock_pa_kernel(tc, q, k, v, x, w_proj, b_proj, out):
+    nc = tc.nc
+    with ExitStack() as ctx:
+        keep = ctx.enter_context(tc.tile_pool(name="keep", bufs=1))
+        psum = ctx.enter_context(tc.psum_pool(name="psum", bufs=8))
+
+        q_rows = q.flatten_outer_dims().rearrange("(i p) e -> p i e", p=P)
+        x_rows = x.flatten_outer_dims().rearrange("(i p) n -> p i n", p=P)
+        out_rows = out.flatten_outer_dims().rearrange("(i p) n -> p i n", p=P)
+        k_rows = k.flatten_outer_dims().rearrange("(p t) e -> p t e", t=PACK)
+        v_rows = v.flatten_outer_dims().rearrange("(p t) f -> p t f", t=PACK)
+        w_rows = w_proj.rearrange("(g t p) n -> p g t n", t=PACK, p=P)
+
+        q_raw = keep.tile([P, Q_TILES, E], BF16, name="q_raw")
+        k_raw = keep.tile([P, PACK, E], BF16, name="k_raw")
+        v_raw = keep.tile([P, PACK, E], BF16, name="v_raw")
+        w_raw = keep.tile([P, F_PASSES, PACK, E], BF16, name="w_raw")
+        x_raw = keep.tile([P, Q_TILES, E], BF16, name="x_raw")
+        b_rows = keep.tile([P, E], BF16, name="b_rows")
+
+        qT = keep.tile([P, Q_TILES, E_CHUNKS, P], BF16, name="qT")
+        kT = keep.tile([P, E_CHUNKS, S], BF16, name="kT")
+
+        v_grouped = keep.tile([P, E, PACK], BF16, name="v_grouped", align_bytes=64)
+        v_codes = keep.tile([P, E], U32, name="v_codes", align_bytes=64)
+        v_scales = keep.tile([P, E], U8, name="v_scales", align_bytes=64)
+        w_grouped = keep.tile([P, F_PASSES, E, PACK], BF16, name="w_grouped", align_bytes=64)
+        w_codes = keep.tile([P, F_PASSES, E], U32, name="w_codes", align_bytes=64)
+        w_scales = keep.tile([P, F_PASSES, E], U8, name="w_scales", align_bytes=64)
+
+        e_bf = keep.tile([P, Q_TILES, S], BF16, name="e_bf")
+        e_grouped = keep.tile([P, Q_TILES, P, PACK], BF16, name="e_grouped", align_bytes=64)
+        e_codes = keep.tile([P, Q_TILES, P], U32, name="e_codes", align_bytes=64)
+        e_scales = keep.tile([P, Q_TILES, P], U8, name="e_scales", align_bytes=64)
+
+        attn_grouped = keep.tile([P, Q_TILES, F_PASSES, P, PACK], BF16, name="attn_grouped", align_bytes=64)
+        attn_codes = keep.tile([P, Q_TILES, F_PASSES, P], U32, name="attn_codes", align_bytes=64)
+        attn_scales = keep.tile([P, Q_TILES, F_PASSES, P], U8, name="attn_scales", align_bytes=64)
+
+        row_max = keep.tile([P, Q_TILES], F32, name="row_max")
+        exp_bias = keep.tile([P, Q_TILES], F32, name="exp_bias")
+        row_sum = keep.tile([P, Q_TILES], F32, name="row_sum")
+        row_inv = keep.tile([P, Q_TILES], F32, name="row_inv")
+        inv_repeated = keep.tile([P, Q_TILES, P], F32, name="inv_repeated")
+        inv_spread = keep.tile([P, Q_TILES, P], F32, name="inv_spread")
+
+        b_spread = keep.tile([P, E], BF16, name="b_spread")
+        x_plus_b = keep.tile([P, Q_TILES, E], F32, name="x_plus_b")
+        out_sb = keep.tile([P, Q_TILES, E], F32, name="out_sb")
+
+        ident_bf = keep.tile([P, P], BF16, name="ident_bf")
+        ident_f32 = keep.tile([P, P], F32, name="ident_f32")
+        ones_bf = keep.tile([P, P], BF16, name="ones_bf")
+        ones_f32 = keep.tile([P, P], F32, name="ones_f32")
+
+        make_identity(nc, ident_bf[:])
+        make_identity(nc, ident_f32[:])
+        nc.vector.memset(b_rows[:], 0.0)
+        nc.vector.memset(ones_bf[:], 1.0)
+        nc.vector.memset(ones_f32[:], 1.0)
+
+        def half(h):
+            return slice(h * BANK, (h + 1) * BANK)
+
+        nc.scalar.dma_start(out=b_rows[0:1, :], in_=b_proj.rearrange("(o n) -> o n", o=1))
+        nc.sync.dma_start(out=q_raw[:, 0, :], in_=q_rows[:, 0, :])
+        for h in range(HALVES):
+            nc.sync.dma_start(out=k_raw[:, :, half(h)], in_=k_rows[:, :, half(h)])
+        for h in range(HALVES):
+            nc.sync.dma_start(out=v_raw[:, :, half(h)], in_=v_rows[:, :, half(h)])
+        nc.sync.dma_start(out=q_raw[:, 1, :], in_=q_rows[:, 1, :])
+        for g in range(F_PASSES):
+            nc.sync.dma_start(out=w_raw[:, g, :, half(0)], in_=w_rows[:, g, :, half(0)])
+            nc.sync.dma_start(out=q_raw[:, 2 + g, :], in_=q_rows[:, 2 + g, :])
+        for g in range(F_PASSES):
+            nc.sync.dma_start(out=w_raw[:, g, :, half(1)], in_=w_rows[:, g, :, half(1)])
+        nc.sync.dma_start(out=x_raw[:], in_=x_rows)
+
+        def copy_on(engine_index, dst, src):
+            if engine_index % 2 == 0:
+                nc.vector.tensor_copy(out=dst, in_=src)
+            else:
+                nc.scalar.copy(out=dst, in_=src)
+
+        def transpose_four(blocks, dst, engine_index):
+            bank = psum.tile([P, PACK, P], BF16, name="t_bank", tag="bank")
+            for j in range(PACK):
+                nc.tensor.transpose(bank[:, j, :], blocks[j], ident_bf[:])
+            copy_on(engine_index, dst, bank[:])
+
+        def transpose_q(i, h):
+            blocks = [q_raw[:, i, c * P : (c + 1) * P] for c in range(h * PACK, (h + 1) * PACK)]
+            transpose_four(blocks, qT[:, i, h * PACK : (h + 1) * PACK, :], h if i == 0 else 1)
+
+        def transpose_k(c):
+            blocks = [k_raw[:, t, c * P : (c + 1) * P] for t in range(PACK)]
+            transpose_four(blocks, kT[:, c, :].rearrange("p (t r) -> p t r", t=PACK), c if c < 4 else 1)
+
+        def regroup(engine_index, grouped, raw):
+            copy_on(
+                engine_index,
+                grouped.rearrange("p (c i) t -> p c t i", i=4),
+                raw.rearrange("p t (c i) -> p c t i", i=4),
+            )
+
+        def quantise(codes, scales, grouped):
+            nc.vector.quantize_mx(out=codes.bitcast(FP8X4), scales=scales, in_=grouped)
+
+        def regroup_v(h):
+            regroup(0, v_grouped[:, half(h), :], v_raw[:, :, half(h)])
+
+        def quantise_v(h):
+            quantise(v_codes[:, half(h)], v_scales[:, half(h)], v_grouped[:, half(h), :].rearrange("p c t -> p (c t)"))
+
+        def regroup_w(h, g, j):
+            cols = slice(h * BANK + j * 256, h * BANK + (j + 1) * 256)
+            regroup(h, w_grouped[:, g, cols, :], w_raw[:, g, :, cols])
+
+        def quantise_w(h, g):
+            quantise(
+                w_codes[:, g, half(h)], w_scales[:, g, half(h)], w_grouped[:, g, half(h), :].rearrange("p c t -> p (c t)")
+            )
+
+        s_banks = {}
+
+        def score_matmul(i, c):
+            if c == 0:
+                s_banks[i] = psum.tile([P, S], F32, name="s_bank", tag="bank")
+            nc.tensor.matmul(
+                s_banks[i][:], lhsT=qT[:, i, c, :], rhs=kT[:, c, :], start=(c == 0), stop=(c == E_CHUNKS - 1)
+            )
+
+        def softmax_max(i):
+            one = slice(i, i + 1)
+            nc.vector.reduce_max(out=row_max[:, one], in_=s_banks[i][:], axis=AXIS.X)
+
+        def softmax_exp(i):
+            one = slice(i, i + 1)
+            nc.scalar.mul(out=exp_bias[:, one], in_=row_max[:, one], mul=-SCORE_SCALE)
+            nc.scalar.activation(
+                out=e_bf[:, i, :],
+                in_=s_banks[i][:],
+                func=ACT.Exp,
+                bias=exp_bias[:, one],
+                scale=SCORE_SCALE,
+                accum_out=row_sum[:, one],
+            )
+
+        def softmax_inv(i):
+            one = slice(i, i + 1)
+            nc.vector.reciprocal(out=row_inv[:, one], in_=row_sum[:, one])
+            nc.scalar.activation(out=inv_repeated[:, i, :], in_=ones_f32[:], func=ACT.Copy, scale=row_inv[:, one])
+
+        def transpose_e(i):
+            bank = psum.tile([P, PACK, P], BF16, name="e_bank", tag="bank")
+            for t in range(PACK):
+                nc.tensor.transpose(bank[:, t, :], e_bf[:, i, t * P : (t + 1) * P], ident_bf[:])
+            nc.scalar.copy(out=e_grouped[:, i, :, :], in_=bank[:].rearrange("p t r -> p r t"))
+            inv_bank = psum.tile([P, P], F32, name="inv_bank", tag="bank")
+            nc.tensor.transpose(inv_bank[:], inv_repeated[:, i, :], ident_f32[:])
+            nc.scalar.copy(out=inv_spread[:, i, :], in_=inv_bank[:])
+
+        def quantise_e(i):
+            quantise(e_codes[:, i, :], e_scales[:, i, :], e_grouped[:, i, :, :].rearrange("p r t -> p (r t)"))
+
+        a_banks = {}
+
+        def attend(i):
+            for g in range(F_PASSES):
+                a_banks[i, g] = psum.tile([P, PACK, P], F32, name="a_bank", tag="bank")
+                for t in range(PACK):
+                    f_cols = slice((g * PACK + t) * P, (g * PACK + t + 1) * P)
+                    nc.tensor.matmul_mx(
+                        out=a_banks[i, g][:, t, :],
+                        lhsT=v_codes[:, f_cols].bitcast(FP8X4),
+                        lhsT_scale=v_scales[:, f_cols],
+                        rhs=e_codes[:, i, :].bitcast(FP8X4),
+                        rhs_scale=e_scales[:, i, :],
+                        start=True,
+                        stop=True,
+                    )
+
+        def normalise(i):
+            for g in range(F_PASSES):
+                nc.vector.tensor_tensor(
+                    out=attn_grouped[:, i, g, :, :],
+                    in0=a_banks[i, g][:].rearrange("p t r -> p r t"),
+                    in1=inv_spread[:, i, :].unsqueeze(2).to_broadcast([P, P, PACK]),
+                    op=ALU.mult,
+                )
+
+        def quantise_attn(i):
+            quantise(
+                attn_codes[:, i, :, :].rearrange("p g r -> p (g r)"),
+                attn_scales[:, i, :, :].rearrange("p g r -> p (g r)"),
+                attn_grouped[:, i, :, :, :].rearrange("p g r t -> p (g r t)"),
+            )
+
+        o_banks = {}
+
+        def project(i, h):
+            o_banks[i, h] = psum.tile([P, BANK], F32, name="o_bank", tag="bank")
+            for g in range(F_PASSES):
+                nc.tensor.matmul_mx(
+                    out=o_banks[i, h][:],
+                    lhsT=attn_codes[:, i, g, :].bitcast(FP8X4),
+                    lhsT_scale=attn_scales[:, i, g, :],
+                    rhs=w_codes[:, g, half(h)].bitcast(FP8X4),
+                    rhs_scale=w_scales[:, g, half(h)],
+                    start=(g == 0),
+                    stop=(g == F_PASSES - 1),
+                )
+
+        def finish(i, h):
+            nc.vector.tensor_tensor(
+                out=out_sb[:, i, half(h)], in0=o_banks[i, h][:], in1=x_plus_b[:, i, half(h)], op=ALU.add
+            )
+            nc.sync.dma_start(out=out_rows[:, i, half(h)], in_=out_sb[:, i, half(h)])
+
+        def spread_b():
+            for h in range(HALVES):
+                b_bank = psum.tile([P, BANK], F32, name="b_bank", tag="bank")
+                nc.tensor.matmul(b_bank[:], lhsT=ones_bf[:], rhs=b_rows[:, half(h)], start=True, stop=True)
+                nc.scalar.copy(out=b_spread[:, half(h)], in_=b_bank[:])
+
+        def add_x_b(i):
+            nc.gpsimd.tensor_tensor(out=x_plus_b[:, i, :], in0=x_raw[:, i, :], in1=b_spread[:], op=ALU.add)
+
+        def live(i):
+            return 0 <= i < Q_TILES
+
+        with tc.manual_schedule():
+            transpose_q(0, 0)
+            transpose_q(0, 1)
+            for c in range(4):
+                transpose_k(c)
+            for r in range(Q_TILES + 3):
+                if live(r):
+                    for c in range(E_CHUNKS):
+                        if r == 0 and c + 4 < E_CHUNKS:
+                            transpose_k(c + 4)
+                        if live(r + 1) and c >= E_CHUNKS - HALVES:
+                            transpose_q(r + 1, c - (E_CHUNKS - HALVES))
+                        score_matmul(r, c)
+                if r == 0:
+                    spread_b()
+                    regroup_v(0)
+                    regroup_v(1)
+                    quantise_v(0)
+                    quantise_v(1)
+                if live(r - 1):
+                    transpose_e(r - 1)
+                if live(r - 2):
+                    attend(r - 2)
+                if live(r):
+                    softmax_max(r)
+                    softmax_exp(r)
+                if live(r - 2):
+                    normalise(r - 2)
+                    quantise_attn(r - 2)
+                if live(r - 1):
+                    quantise_e(r - 1)
+                if r == 0:
+                    regroup_w(0, 0, 0)
+                    regroup_w(0, 0, 1)
+                if live(r):
+                    softmax_inv(r)
+                if live(r - 3):
+                    for h in range(HALVES):
+                        project(r - 3, h)
+                    for h in range(HALVES):
+                        finish(r - 3, h)
+                if r == 0:
+                    quantise_w(0, 0)
+                    regroup_w(0, 1, 0)
+                    regroup_w(0, 1, 1)
+                    regroup_w(1, 0, 0)
+                if r == 1:
+                    quantise_w(0, 1)
+                    regroup_w(1, 0, 1)
+                    regroup_w(1, 1, 0)
+                if r == 2:
+                    quantise_w(1, 0)
+                    regroup_w(1, 1, 1)
+                    quantise_w(1, 1)
+                    for i in range(Q_TILES):
+                        add_x_b(i)

@@ -19,6 +19,7 @@ E = 1024
 HEAD = 64
 BANK = 512
 SCORE_SCALE = HEAD**-0.5
+XB_PIECE = 256
 
 Q_TILES = S // P
 E_CHUNKS = E // P
@@ -254,7 +255,9 @@ def tile_transformerblock_pa_kernel(tc, q, k, v, x, w_proj, b_proj, out):
                 nc.scalar.copy(out=b_spread[:, half(h)], in_=b_bank[:])
 
         def add_x_b(i):
-            nc.gpsimd.tensor_tensor(out=x_plus_b[:, i, :], in0=x_raw[:, i, :], in1=b_spread[:], op=ALU.add)
+            for j in range(E // XB_PIECE):
+                cols = slice(j * XB_PIECE, (j + 1) * XB_PIECE)
+                nc.gpsimd.tensor_tensor(out=x_plus_b[:, i, cols], in0=x_raw[:, i, cols], in1=b_spread[:, cols], op=ALU.add)
 
         def live(i):
             return 0 <= i < Q_TILES

@@ -19,12 +19,15 @@ E = 1024
 HEAD = 64
 BANK = 512
 SCORE_SCALE = HEAD**-0.5
-XB_PIECE = 256
 
 Q_TILES = S // P
 E_CHUNKS = E // P
+WORD_CHUNKS = E // (2 * P)
 F_PASSES = E // (P * PACK)
 HALVES = E // BANK
+K_AHEAD = 2
+XB_PIECE = 256
+W_SHARE = BANK // 2
 
 FLOPS = 2 * S * S * E + 2 * S * S * E + 2 * S * E * E
 
@@ -49,8 +52,8 @@ def tile_transformerblock_pa_kernel(tc, q, k, v, x, w_proj, b_proj, out):
         x_raw = keep.tile([P, Q_TILES, E], BF16, name="x_raw")
         b_rows = keep.tile([P, E], BF16, name="b_rows")
 
-        qT = keep.tile([P, Q_TILES, E_CHUNKS, P], BF16, name="qT")
-        kT = keep.tile([P, E_CHUNKS, S], BF16, name="kT")
+        qT = keep.tile([P, Q_TILES, WORD_CHUNKS, P, 2], BF16, name="qT")
+        kT = keep.tile([P, WORD_CHUNKS, S, 2], BF16, name="kT")
 
         v_grouped = keep.tile([P, E, PACK], BF16, name="v_grouped", align_bytes=64)
         v_codes = keep.tile([P, E], U32, name="v_codes", align_bytes=64)
@@ -83,17 +86,22 @@ def tile_transformerblock_pa_kernel(tc, q, k, v, x, w_proj, b_proj, out):
         ident_f32 = keep.tile([P, P], F32, name="ident_f32")
         ones_bf = keep.tile([P, P], BF16, name="ones_bf")
         ones_f32 = keep.tile([P, P], F32, name="ones_f32")
-
-        make_identity(nc, ident_bf[:])
-        make_identity(nc, ident_f32[:])
-        nc.vector.memset(b_rows[:], 0.0)
-        nc.vector.memset(ones_bf[:], 1.0)
-        nc.vector.memset(ones_f32[:], 1.0)
+        table_warm = keep.tile([P, 1], F32, name="table_warm")
 
         def half(h):
             return slice(h * BANK, (h + 1) * BANK)
 
-        nc.scalar.dma_start(out=b_rows[0:1, :], in_=b_proj.rearrange("(o n) -> o n", o=1))
+        def live(i):
+            return 0 <= i < Q_TILES
+
+        make_identity(nc, ident_f32[:])
+        make_identity(nc, ident_bf[:])
+        nc.vector.memset(b_rows[:], 0.0)
+        nc.vector.memset(ones_bf[:], 1.0)
+        nc.vector.memset(ones_f32[:], 1.0)
+        nc.scalar.activation(out=table_warm[:], in_=ones_f32[:, 0:1], func=ACT.Exp)
+
+        nc.sync.dma_start(out=b_rows[0:1, :], in_=b_proj.rearrange("(o n) -> o n", o=1))
         nc.sync.dma_start(out=q_raw[:, 0, :], in_=q_rows[:, 0, :])
         for h in range(HALVES):
             nc.sync.dma_start(out=k_raw[:, :, half(h)], in_=k_rows[:, :, half(h)])
@@ -107,63 +115,77 @@ def tile_transformerblock_pa_kernel(tc, q, k, v, x, w_proj, b_proj, out):
             nc.sync.dma_start(out=w_raw[:, g, :, half(1)], in_=w_rows[:, g, :, half(1)])
         nc.sync.dma_start(out=x_raw[:], in_=x_rows)
 
-        def copy_on(engine_index, dst, src):
-            if engine_index % 2 == 0:
-                nc.vector.tensor_copy(out=dst, in_=src)
-            else:
-                nc.scalar.copy(out=dst, in_=src)
+        def spread_b():
+            for h in range(HALVES):
+                b_bank = psum.tile([P, BANK], F32, name="b_bank", tag="bank")
+                nc.tensor.matmul(b_bank[:], lhsT=ones_bf[:], rhs=b_rows[:, half(h)], start=True, stop=True)
+                nc.vector.tensor_copy(out=b_spread[:, half(h)], in_=b_bank[:])
 
-        def transpose_four(blocks, dst, engine_index):
-            bank = psum.tile([P, PACK, P], BF16, name="t_bank", tag="bank")
+        def add_x_b(i):
+            for j in range(E // XB_PIECE):
+                cols = slice(j * XB_PIECE, (j + 1) * XB_PIECE)
+                nc.gpsimd.tensor_tensor(out=x_plus_b[:, i, cols], in0=x_raw[:, i, cols], in1=b_spread[:, cols], op=ALU.add)
+
+        def transpose_words(blocks, dst, copy):
+            bank = psum.tile([P, PACK, P], F32, name="t_bank", tag="bank")
             for j in range(PACK):
-                nc.tensor.transpose(bank[:, j, :], blocks[j], ident_bf[:])
-            copy_on(engine_index, dst, bank[:])
+                nc.tensor.transpose(bank[:, j, :], blocks[j], ident_f32[:])
+            copy(out=dst, in_=bank[:].rearrange("p j r -> p (j r)"))
 
-        def transpose_q(i, h):
-            blocks = [q_raw[:, i, c * P : (c + 1) * P] for c in range(h * PACK, (h + 1) * PACK)]
-            transpose_four(blocks, qT[:, i, h * PACK : (h + 1) * PACK, :], h if i == 0 else 1)
+        def transpose_q(i, copy):
+            words = q_raw[:, i, :].bitcast(F32)
+            blocks = [words[:, u * P : (u + 1) * P] for u in range(WORD_CHUNKS)]
+            transpose_words(blocks, qT[:, i].rearrange("p u r e -> p (u r e)").bitcast(F32), copy)
 
-        def transpose_k(c):
-            blocks = [k_raw[:, t, c * P : (c + 1) * P] for t in range(PACK)]
-            transpose_four(blocks, kT[:, c, :].rearrange("p (t r) -> p t r", t=PACK), c if c < 4 else 1)
+        def transpose_k(u):
+            blocks = [k_raw[:, t, :].bitcast(F32)[:, u * P : (u + 1) * P] for t in range(PACK)]
+            transpose_words(blocks, kT[:, u].rearrange("p s e -> p (s e)").bitcast(F32), nc.scalar.copy)
 
-        def regroup(engine_index, grouped, raw):
-            copy_on(
-                engine_index,
-                grouped.rearrange("p (c i) t -> p c t i", i=4),
-                raw.rearrange("p t (c i) -> p c t i", i=4),
+        def regroup(copy, grouped, raw):
+            copy(
+                out=grouped.rearrange("p (c i) t -> p c t i", i=4),
+                in_=raw.rearrange("p t (c i) -> p c t i", i=4),
             )
 
         def quantise(codes, scales, grouped):
             nc.vector.quantize_mx(out=codes.bitcast(FP8X4), scales=scales, in_=grouped)
 
         def regroup_v(h):
-            regroup(0, v_grouped[:, half(h), :], v_raw[:, :, half(h)])
+            regroup(nc.vector.tensor_copy, v_grouped[:, half(h), :], v_raw[:, :, half(h)])
 
         def quantise_v(h):
             quantise(v_codes[:, half(h)], v_scales[:, half(h)], v_grouped[:, half(h), :].rearrange("p c t -> p (c t)"))
 
-        def regroup_w(h, g, j):
-            cols = slice(h * BANK + j * 256, h * BANK + (j + 1) * 256)
-            regroup(h, w_grouped[:, g, cols, :], w_raw[:, g, :, cols])
+        def w_piece(r):
+            return r // F_PASSES, r % F_PASSES
 
-        def quantise_w(h, g):
+        def regroup_w(r, copy, first):
+            h, g = w_piece(r)
+            cols = slice(h * BANK + first, h * BANK + first + W_SHARE)
+            regroup(copy, w_grouped[:, g, cols, :], w_raw[:, g, :, cols])
+
+        def quantise_w(r):
+            h, g = w_piece(r)
             quantise(
                 w_codes[:, g, half(h)], w_scales[:, g, half(h)], w_grouped[:, g, half(h), :].rearrange("p c t -> p (c t)")
             )
 
         s_banks = {}
+        a_banks = {}
 
         def score_matmul(i, c):
             if c == 0:
                 s_banks[i] = psum.tile([P, S], F32, name="s_bank", tag="bank")
             nc.tensor.matmul(
-                s_banks[i][:], lhsT=qT[:, i, c, :], rhs=kT[:, c, :], start=(c == 0), stop=(c == E_CHUNKS - 1)
+                s_banks[i][:],
+                lhsT=qT[:, i, c // 2, :, c % 2],
+                rhs=kT[:, c // 2, :, c % 2],
+                start=(c == 0),
+                stop=(c == E_CHUNKS - 1),
             )
 
         def softmax_max(i):
-            one = slice(i, i + 1)
-            nc.vector.reduce_max(out=row_max[:, one], in_=s_banks[i][:], axis=AXIS.X)
+            nc.vector.reduce_max(out=row_max[:, i : i + 1], in_=s_banks[i][:], axis=AXIS.X)
 
         def softmax_exp(i):
             one = slice(i, i + 1)
@@ -187,14 +209,14 @@ def tile_transformerblock_pa_kernel(tc, q, k, v, x, w_proj, b_proj, out):
             for t in range(PACK):
                 nc.tensor.transpose(bank[:, t, :], e_bf[:, i, t * P : (t + 1) * P], ident_bf[:])
             nc.scalar.copy(out=e_grouped[:, i, :, :], in_=bank[:].rearrange("p t r -> p r t"))
-            inv_bank = psum.tile([P, P], F32, name="inv_bank", tag="bank")
-            nc.tensor.transpose(inv_bank[:], inv_repeated[:, i, :], ident_f32[:])
-            nc.scalar.copy(out=inv_spread[:, i, :], in_=inv_bank[:])
 
         def quantise_e(i):
             quantise(e_codes[:, i, :], e_scales[:, i, :], e_grouped[:, i, :, :].rearrange("p r t -> p (r t)"))
 
-        a_banks = {}
+        def spread_inv(i):
+            inv_bank = psum.tile([P, P], F32, name="inv_bank", tag="bank")
+            nc.tensor.transpose(inv_bank[:], inv_repeated[:, i, :], ident_f32[:])
+            nc.scalar.copy(out=inv_spread[:, i, :], in_=inv_bank[:])
 
         def attend(i):
             for g in range(F_PASSES):
@@ -227,94 +249,63 @@ def tile_transformerblock_pa_kernel(tc, q, k, v, x, w_proj, b_proj, out):
                 attn_grouped[:, i, :, :, :].rearrange("p g r t -> p (g r t)"),
             )
 
-        o_banks = {}
-
-        def project(i, h):
-            o_banks[i, h] = psum.tile([P, BANK], F32, name="o_bank", tag="bank")
-            for g in range(F_PASSES):
-                nc.tensor.matmul_mx(
-                    out=o_banks[i, h][:],
-                    lhsT=attn_codes[:, i, g, :].bitcast(FP8X4),
-                    lhsT_scale=attn_scales[:, i, g, :],
-                    rhs=w_codes[:, g, half(h)].bitcast(FP8X4),
-                    rhs_scale=w_scales[:, g, half(h)],
-                    start=(g == 0),
-                    stop=(g == F_PASSES - 1),
-                )
-
-        def finish(i, h):
-            nc.vector.tensor_tensor(
-                out=out_sb[:, i, half(h)], in0=o_banks[i, h][:], in1=x_plus_b[:, i, half(h)], op=ALU.add
-            )
-            nc.sync.dma_start(out=out_rows[:, i, half(h)], in_=out_sb[:, i, half(h)])
-
-        def spread_b():
+        def project(i):
             for h in range(HALVES):
-                b_bank = psum.tile([P, BANK], F32, name="b_bank", tag="bank")
-                nc.tensor.matmul(b_bank[:], lhsT=ones_bf[:], rhs=b_rows[:, half(h)], start=True, stop=True)
-                nc.scalar.copy(out=b_spread[:, half(h)], in_=b_bank[:])
-
-        def add_x_b(i):
-            for j in range(E // XB_PIECE):
-                cols = slice(j * XB_PIECE, (j + 1) * XB_PIECE)
-                nc.gpsimd.tensor_tensor(out=x_plus_b[:, i, cols], in0=x_raw[:, i, cols], in1=b_spread[:, cols], op=ALU.add)
-
-        def live(i):
-            return 0 <= i < Q_TILES
+                o_bank = psum.tile([P, BANK], F32, name="o_bank", tag="bank")
+                for g in range(F_PASSES):
+                    nc.tensor.matmul_mx(
+                        out=o_bank[:],
+                        lhsT=attn_codes[:, i, g, :].bitcast(FP8X4),
+                        lhsT_scale=attn_scales[:, i, g, :],
+                        rhs=w_codes[:, g, half(h)].bitcast(FP8X4),
+                        rhs_scale=w_scales[:, g, half(h)],
+                        start=(g == 0),
+                        stop=(g == F_PASSES - 1),
+                    )
+                nc.vector.tensor_tensor(out=out_sb[:, i, half(h)], in0=o_bank[:], in1=x_plus_b[:, i, half(h)], op=ALU.add)
+                nc.sync.dma_start(out=out_rows[:, i, half(h)], in_=out_sb[:, i, half(h)])
 
         with tc.manual_schedule():
-            transpose_q(0, 0)
-            transpose_q(0, 1)
-            for c in range(4):
-                transpose_k(c)
-            for r in range(Q_TILES + 3):
+            spread_b()
+            transpose_q(0, nc.vector.tensor_copy)
+            for u in range(K_AHEAD):
+                transpose_k(u)
+            for r in range(Q_TILES + 2):
                 if live(r):
                     for c in range(E_CHUNKS):
-                        if r == 0 and c + 4 < E_CHUNKS:
-                            transpose_k(c + 4)
-                        if live(r + 1) and c >= E_CHUNKS - HALVES:
-                            transpose_q(r + 1, c - (E_CHUNKS - HALVES))
+                        if r == 0 and c % 2 == 0 and c // 2 + K_AHEAD < WORD_CHUNKS:
+                            transpose_k(c // 2 + K_AHEAD)
+                        if c == E_CHUNKS - 2 and live(r + 1):
+                            transpose_q(r + 1, nc.scalar.copy)
                         score_matmul(r, c)
                 if r == 0:
-                    spread_b()
                     regroup_v(0)
                     regroup_v(1)
                     quantise_v(0)
-                    quantise_v(1)
                 if live(r - 1):
                     transpose_e(r - 1)
                 if live(r - 2):
+                    spread_inv(r - 2)
                     attend(r - 2)
                 if live(r):
                     softmax_max(r)
+                    regroup_w(r, nc.scalar.copy, W_SHARE)
                     softmax_exp(r)
+                if r == 0:
+                    quantise_v(1)
                 if live(r - 2):
                     normalise(r - 2)
-                    quantise_attn(r - 2)
                 if live(r - 1):
                     quantise_e(r - 1)
-                if r == 0:
-                    regroup_w(0, 0, 0)
-                    regroup_w(0, 0, 1)
                 if live(r):
+                    regroup_w(r, nc.vector.tensor_copy, 0)
                     softmax_inv(r)
-                if live(r - 3):
-                    for h in range(HALVES):
-                        project(r - 3, h)
-                    for h in range(HALVES):
-                        finish(r - 3, h)
-                if r == 0:
-                    quantise_w(0, 0)
-                    regroup_w(0, 1, 0)
-                    regroup_w(0, 1, 1)
-                    regroup_w(1, 0, 0)
-                if r == 1:
-                    quantise_w(0, 1)
-                    regroup_w(1, 0, 1)
-                    regroup_w(1, 1, 0)
+                if live(r - 2):
+                    quantise_attn(r - 2)
+                if live(r - 1):
+                    quantise_w(r - 1)
                 if r == 2:
-                    quantise_w(1, 0)
-                    regroup_w(1, 1, 1)
-                    quantise_w(1, 1)
                     for i in range(Q_TILES):
                         add_x_b(i)
+            for i in range(Q_TILES):
+                project(i)

@@ -25,9 +25,11 @@ E_CHUNKS = E // P
 WORD_CHUNKS = E // (2 * P)
 F_PASSES = E // (P * PACK)
 HALVES = E // BANK
+WARM_UPS = 4
+Q_TURNS = ((0, 4), (1, 2), (1, 4))
 K_AHEAD = 2
 XB_PIECE = 256
-W_SHARE = BANK // 2
+V_SHARE = BANK // 4
 
 FLOPS = 2 * S * S * E + 2 * S * S * E + 2 * S * E * E
 
@@ -46,9 +48,9 @@ def tile_transformerblock_pa_kernel(tc, q, k, v, x, w_proj, b_proj, out):
         w_rows = w_proj.rearrange("(g t p) n -> p g t n", t=PACK, p=P)
 
         q_raw = keep.tile([P, Q_TILES, E], BF16, name="q_raw")
-        k_raw = keep.tile([P, PACK, E], BF16, name="k_raw")
-        v_raw = keep.tile([P, PACK, E], BF16, name="v_raw")
-        w_raw = keep.tile([P, F_PASSES, PACK, E], BF16, name="w_raw")
+        k_raw = [keep.tile([P, PACK, BANK], BF16, name=f"k_raw{h}") for h in range(HALVES)]
+        v_raw = [keep.tile([P, PACK, BANK], BF16, name=f"v_raw{h}") for h in range(HALVES)]
+        w_raw = [keep.tile([P, PACK, BANK], BF16, name=f"w_raw{r}") for r in range(HALVES * F_PASSES)]
         x_raw = keep.tile([P, Q_TILES, E], BF16, name="x_raw")
         b_rows = keep.tile([P, E], BF16, name="b_rows")
 
@@ -75,7 +77,6 @@ def tile_transformerblock_pa_kernel(tc, q, k, v, x, w_proj, b_proj, out):
         exp_bias = keep.tile([P, Q_TILES], F32, name="exp_bias")
         row_sum = keep.tile([P, Q_TILES], F32, name="row_sum")
         row_inv = keep.tile([P, Q_TILES], F32, name="row_inv")
-        inv_repeated = keep.tile([P, Q_TILES, P], F32, name="inv_repeated")
         inv_spread = keep.tile([P, Q_TILES, P], F32, name="inv_spread")
 
         b_spread = keep.tile([P, E], BF16, name="b_spread")
@@ -86,6 +87,7 @@ def tile_transformerblock_pa_kernel(tc, q, k, v, x, w_proj, b_proj, out):
         ident_f32 = keep.tile([P, P], F32, name="ident_f32")
         ones_bf = keep.tile([P, P], BF16, name="ones_bf")
         ones_f32 = keep.tile([P, P], F32, name="ones_f32")
+        warm = keep.tile([P, BANK], BF16, name="warm")
         table_warm = keep.tile([P, 1], F32, name="table_warm")
 
         def half(h):
@@ -96,30 +98,36 @@ def tile_transformerblock_pa_kernel(tc, q, k, v, x, w_proj, b_proj, out):
 
         make_identity(nc, ident_f32[:])
         make_identity(nc, ident_bf[:])
+        nc.vector.memset(warm[:], 0.0)
         nc.vector.memset(b_rows[:], 0.0)
         nc.vector.memset(ones_bf[:], 1.0)
         nc.vector.memset(ones_f32[:], 1.0)
         nc.scalar.activation(out=table_warm[:], in_=ones_f32[:, 0:1], func=ACT.Exp)
 
-        nc.sync.dma_start(out=b_rows[0:1, :], in_=b_proj.rearrange("(o n) -> o n", o=1))
         nc.sync.dma_start(out=q_raw[:, 0, :], in_=q_rows[:, 0, :])
         for h in range(HALVES):
-            nc.sync.dma_start(out=k_raw[:, :, half(h)], in_=k_rows[:, :, half(h)])
-        for h in range(HALVES):
-            nc.sync.dma_start(out=v_raw[:, :, half(h)], in_=v_rows[:, :, half(h)])
+            nc.sync.dma_start(out=k_raw[h][:], in_=k_rows[:, :, half(h)])
+        nc.sync.dma_start(out=b_rows[0:1, :], in_=b_proj.rearrange("(o n) -> o n", o=1))
         nc.sync.dma_start(out=q_raw[:, 1, :], in_=q_rows[:, 1, :])
-        for g in range(F_PASSES):
-            nc.sync.dma_start(out=w_raw[:, g, :, half(0)], in_=w_rows[:, g, :, half(0)])
-            nc.sync.dma_start(out=q_raw[:, 2 + g, :], in_=q_rows[:, 2 + g, :])
-        for g in range(F_PASSES):
-            nc.sync.dma_start(out=w_raw[:, g, :, half(1)], in_=w_rows[:, g, :, half(1)])
+        for h in range(HALVES):
+            nc.sync.dma_start(out=v_raw[h][:], in_=v_rows[:, :, half(h)])
+        for i in range(2, Q_TILES):
+            nc.sync.dma_start(out=q_raw[:, i, :], in_=q_rows[:, i, :])
+        for h in range(HALVES):
+            for g in range(F_PASSES):
+                nc.sync.dma_start(out=w_raw[h * F_PASSES + g][:], in_=w_rows[:, g, :, half(h)])
         nc.sync.dma_start(out=x_raw[:], in_=x_rows)
 
         def spread_b():
             for h in range(HALVES):
                 b_bank = psum.tile([P, BANK], F32, name="b_bank", tag="bank")
                 nc.tensor.matmul(b_bank[:], lhsT=ones_bf[:], rhs=b_rows[:, half(h)], start=True, stop=True)
-                nc.vector.tensor_copy(out=b_spread[:, half(h)], in_=b_bank[:])
+                nc.scalar.copy(out=b_spread[:, half(h)], in_=b_bank[:])
+
+        def warm_up():
+            bank = psum.tile([P, BANK], F32, name="warm_bank", tag="bank")
+            for n in range(WARM_UPS):
+                nc.tensor.matmul(bank[:], lhsT=warm[:, 0:P], rhs=warm[:], start=True, stop=True)
 
         def add_x_b(i):
             for j in range(E // XB_PIECE):
@@ -137,9 +145,10 @@ def tile_transformerblock_pa_kernel(tc, q, k, v, x, w_proj, b_proj, out):
             blocks = [words[:, u * P : (u + 1) * P] for u in range(WORD_CHUNKS)]
             transpose_words(blocks, qT[:, i].rearrange("p u r e -> p (u r e)").bitcast(F32), copy)
 
-        def transpose_k(u):
-            blocks = [k_raw[:, t, :].bitcast(F32)[:, u * P : (u + 1) * P] for t in range(PACK)]
-            transpose_words(blocks, kT[:, u].rearrange("p s e -> p (s e)").bitcast(F32), nc.scalar.copy)
+        def transpose_k(u, copy):
+            h, first = u // HALVES, u % HALVES * P
+            blocks = [k_raw[h][:, t, :].bitcast(F32)[:, first : first + P] for t in range(PACK)]
+            transpose_words(blocks, kT[:, u].rearrange("p s e -> p (s e)").bitcast(F32), copy)
 
         def regroup(copy, grouped, raw):
             copy(
@@ -150,8 +159,8 @@ def tile_transformerblock_pa_kernel(tc, q, k, v, x, w_proj, b_proj, out):
         def quantise(codes, scales, grouped):
             nc.vector.quantize_mx(out=codes.bitcast(FP8X4), scales=scales, in_=grouped)
 
-        def regroup_v(h):
-            regroup(nc.vector.tensor_copy, v_grouped[:, half(h), :], v_raw[:, :, half(h)])
+        def regroup_v(h, copy, first, end):
+            regroup(copy, v_grouped[:, h * BANK + first : h * BANK + end, :], v_raw[h][:, :, first:end])
 
         def quantise_v(h):
             quantise(v_codes[:, half(h)], v_scales[:, half(h)], v_grouped[:, half(h), :].rearrange("p c t -> p (c t)"))
@@ -159,10 +168,9 @@ def tile_transformerblock_pa_kernel(tc, q, k, v, x, w_proj, b_proj, out):
         def w_piece(r):
             return r // F_PASSES, r % F_PASSES
 
-        def regroup_w(r, copy, first):
+        def regroup_w(r, copy, first, end):
             h, g = w_piece(r)
-            cols = slice(h * BANK + first, h * BANK + first + W_SHARE)
-            regroup(copy, w_grouped[:, g, cols, :], w_raw[:, g, :, cols])
+            regroup(copy, w_grouped[:, g, h * BANK + first : h * BANK + end, :], w_raw[r][:, :, first:end])
 
         def quantise_w(r):
             h, g = w_piece(r)
@@ -202,7 +210,6 @@ def tile_transformerblock_pa_kernel(tc, q, k, v, x, w_proj, b_proj, out):
         def softmax_inv(i):
             one = slice(i, i + 1)
             nc.vector.reciprocal(out=row_inv[:, one], in_=row_sum[:, one])
-            nc.scalar.activation(out=inv_repeated[:, i, :], in_=ones_f32[:], func=ACT.Copy, scale=row_inv[:, one])
 
         def transpose_e(i):
             bank = psum.tile([P, PACK, P], BF16, name="e_bank", tag="bank")
@@ -215,7 +222,7 @@ def tile_transformerblock_pa_kernel(tc, q, k, v, x, w_proj, b_proj, out):
 
         def spread_inv(i):
             inv_bank = psum.tile([P, P], F32, name="inv_bank", tag="bank")
-            nc.tensor.transpose(inv_bank[:], inv_repeated[:, i, :], ident_f32[:])
+            nc.tensor.transpose(inv_bank[:], row_inv[:, i : i + 1].to_broadcast([P, P]), ident_f32[:])
             nc.scalar.copy(out=inv_spread[:, i, :], in_=inv_bank[:])
 
         def attend(i):
@@ -265,32 +272,36 @@ def tile_transformerblock_pa_kernel(tc, q, k, v, x, w_proj, b_proj, out):
                 nc.vector.tensor_tensor(out=out_sb[:, i, half(h)], in0=o_bank[:], in1=x_plus_b[:, i, half(h)], op=ALU.add)
                 nc.sync.dma_start(out=out_rows[:, i, half(h)], in_=out_sb[:, i, half(h)])
 
+        k_copies = (nc.scalar.copy, nc.vector.tensor_copy)
         with tc.manual_schedule():
-            spread_b()
+            warm_up()
             transpose_q(0, nc.vector.tensor_copy)
             for u in range(K_AHEAD):
-                transpose_k(u)
+                transpose_k(u, k_copies[u % 2])
             for r in range(Q_TILES + 2):
-                if live(r):
-                    for c in range(E_CHUNKS):
-                        if r == 0 and c % 2 == 0 and c // 2 + K_AHEAD < WORD_CHUNKS:
-                            transpose_k(c // 2 + K_AHEAD)
-                        if c == E_CHUNKS - 2 and live(r + 1):
-                            transpose_q(r + 1, nc.scalar.copy)
-                        score_matmul(r, c)
+                for c in range(E_CHUNKS if live(r) else 0):
+                    if r == 0 and c % 2 == 0 and c // 2 + K_AHEAD < WORD_CHUNKS:
+                        transpose_k(c // 2 + K_AHEAD, nc.scalar.copy)
+                    if (r, c) in Q_TURNS:
+                        transpose_q(Q_TURNS.index((r, c)) + 1, nc.scalar.copy)
+                    if (r, c) == (0, 2):
+                        spread_b()
+                    score_matmul(r, c)
                 if r == 0:
-                    regroup_v(0)
-                    regroup_v(1)
+                    regroup_v(0, nc.vector.tensor_copy, 0, BANK)
+                    regroup_v(1, nc.scalar.copy, BANK // 2, BANK)
+                    regroup_v(1, nc.vector.tensor_copy, 0, BANK // 2)
                     quantise_v(0)
                 if live(r - 1):
                     transpose_e(r - 1)
+                    spread_inv(r - 1)
                 if live(r - 2):
-                    spread_inv(r - 2)
                     attend(r - 2)
                 if live(r):
                     softmax_max(r)
-                    regroup_w(r, nc.scalar.copy, W_SHARE)
                     softmax_exp(r)
+                if live(r - 1):
+                    regroup_w(r - 1, nc.scalar.copy, V_SHARE, BANK)
                 if r == 0:
                     quantise_v(1)
                 if live(r - 2):
@@ -298,12 +309,12 @@ def tile_transformerblock_pa_kernel(tc, q, k, v, x, w_proj, b_proj, out):
                 if live(r - 1):
                     quantise_e(r - 1)
                 if live(r):
-                    regroup_w(r, nc.vector.tensor_copy, 0)
+                    regroup_w(r, nc.vector.tensor_copy, 0, V_SHARE)
                     softmax_inv(r)
                 if live(r - 2):
                     quantise_attn(r - 2)
-                if live(r - 1):
-                    quantise_w(r - 1)
+                if live(r - 2):
+                    quantise_w(r - 2)
                 if r == 2:
                     for i in range(Q_TILES):
                         add_x_b(i)

@@ -26,10 +26,13 @@ WORD_CHUNKS = E // (2 * P)
 F_PASSES = E // (P * PACK)
 HALVES = E // BANK
 WARM_UPS = 4
-Q_TURNS = ((0, 4), (1, 2), (1, 4))
+Q_TURNS = ((0, 4), (1, 0), (1, 3))
 K_AHEAD = 2
 XB_PIECE = 256
-V_SHARE = BANK // 4
+
+S_PARTS = {1: ((2, 0),), 2: ((2, 1),), 3: ((3, 0),), 4: ((3, 1),)}
+V_COLS = (BANK, BANK)
+W_QUANT = {0: (0,), 1: (1,), 3: (2,), 5: (3,)}
 
 FLOPS = 2 * S * S * E + 2 * S * S * E + 2 * S * E * E
 
@@ -86,7 +89,6 @@ def tile_transformerblock_pa_kernel(tc, q, k, v, x, w_proj, b_proj, out):
         ident_bf = keep.tile([P, P], BF16, name="ident_bf")
         ident_f32 = keep.tile([P, P], F32, name="ident_f32")
         ones_bf = keep.tile([P, P], BF16, name="ones_bf")
-        ones_f32 = keep.tile([P, P], F32, name="ones_f32")
         warm = keep.tile([P, BANK], BF16, name="warm")
         table_warm = keep.tile([P, 1], F32, name="table_warm")
 
@@ -98,16 +100,16 @@ def tile_transformerblock_pa_kernel(tc, q, k, v, x, w_proj, b_proj, out):
 
         make_identity(nc, ident_f32[:])
         make_identity(nc, ident_bf[:])
-        nc.vector.memset(warm[:], 0.0)
-        nc.vector.memset(b_rows[:], 0.0)
+        nc.vector.memset(warm[:].bitcast(U32), 0)
+        nc.vector.memset(b_rows[:].bitcast(U32), 0)
         nc.vector.memset(ones_bf[:], 1.0)
-        nc.vector.memset(ones_f32[:], 1.0)
-        nc.scalar.activation(out=table_warm[:], in_=ones_f32[:, 0:1], func=ACT.Exp)
+        nc.scalar.activation(out=table_warm[:], in_=ones_bf[:, 0:1], func=ACT.Exp)
 
         nc.sync.dma_start(out=q_raw[:, 0, :], in_=q_rows[:, 0, :])
         for h in range(HALVES):
             nc.sync.dma_start(out=k_raw[h][:], in_=k_rows[:, :, half(h)])
-        nc.sync.dma_start(out=b_rows[0:1, :], in_=b_proj.rearrange("(o n) -> o n", o=1))
+            if h == 0:
+                nc.sync.dma_start(out=b_rows[0:1, :], in_=b_proj.rearrange("(o n) -> o n", o=1))
         nc.sync.dma_start(out=q_raw[:, 1, :], in_=q_rows[:, 1, :])
         for h in range(HALVES):
             nc.sync.dma_start(out=v_raw[h][:], in_=v_rows[:, :, half(h)])
@@ -116,13 +118,17 @@ def tile_transformerblock_pa_kernel(tc, q, k, v, x, w_proj, b_proj, out):
         for h in range(HALVES):
             for g in range(F_PASSES):
                 nc.sync.dma_start(out=w_raw[h * F_PASSES + g][:], in_=w_rows[:, g, :, half(h)])
-        nc.sync.dma_start(out=x_raw[:], in_=x_rows)
+            tiles = slice(h * Q_TILES // HALVES, (h + 1) * Q_TILES // HALVES)
+            nc.sync.dma_start(out=x_raw[:, tiles, :], in_=x_rows[:, tiles, :])
 
         def spread_b():
             for h in range(HALVES):
-                b_bank = psum.tile([P, BANK], F32, name="b_bank", tag="bank")
-                nc.tensor.matmul(b_bank[:], lhsT=ones_bf[:], rhs=b_rows[:, half(h)], start=True, stop=True)
-                nc.scalar.copy(out=b_spread[:, half(h)], in_=b_bank[:])
+                b_banks[h] = psum.tile([P, BANK], F32, name="b_bank", tag="bank")
+                nc.tensor.matmul(b_banks[h][:], lhsT=ones_bf[:], rhs=b_rows[:, half(h)], start=True, stop=True)
+
+        def copy_b():
+            for h in range(HALVES):
+                nc.scalar.copy(out=b_spread[:, half(h)], in_=b_banks[h][:])
 
         def warm_up():
             bank = psum.tile([P, BANK], F32, name="warm_bank", tag="bank")
@@ -180,6 +186,8 @@ def tile_transformerblock_pa_kernel(tc, q, k, v, x, w_proj, b_proj, out):
 
         s_banks = {}
         a_banks = {}
+        b_banks = {}
+        o_banks = {}
 
         def score_matmul(i, c):
             if c == 0:
@@ -256,21 +264,22 @@ def tile_transformerblock_pa_kernel(tc, q, k, v, x, w_proj, b_proj, out):
                 attn_grouped[:, i, :, :, :].rearrange("p g r t -> p (g r t)"),
             )
 
-        def project(i):
-            for h in range(HALVES):
-                o_bank = psum.tile([P, BANK], F32, name="o_bank", tag="bank")
-                for g in range(F_PASSES):
-                    nc.tensor.matmul_mx(
-                        out=o_bank[:],
-                        lhsT=attn_codes[:, i, g, :].bitcast(FP8X4),
-                        lhsT_scale=attn_scales[:, i, g, :],
-                        rhs=w_codes[:, g, half(h)].bitcast(FP8X4),
-                        rhs_scale=w_scales[:, g, half(h)],
-                        start=(g == 0),
-                        stop=(g == F_PASSES - 1),
-                    )
-                nc.vector.tensor_tensor(out=out_sb[:, i, half(h)], in0=o_bank[:], in1=x_plus_b[:, i, half(h)], op=ALU.add)
-                nc.sync.dma_start(out=out_rows[:, i, half(h)], in_=out_sb[:, i, half(h)])
+        def project(i, h):
+            o_bank = o_banks[i, h] = psum.tile([P, BANK], F32, name="o_bank", tag="bank")
+            for g in range(F_PASSES):
+                nc.tensor.matmul_mx(
+                    out=o_bank[:],
+                    lhsT=attn_codes[:, i, g, :].bitcast(FP8X4),
+                    lhsT_scale=attn_scales[:, i, g, :],
+                    rhs=w_codes[:, g, half(h)].bitcast(FP8X4),
+                    rhs_scale=w_scales[:, g, half(h)],
+                    start=(g == 0),
+                    stop=(g == F_PASSES - 1),
+                )
+
+        def finish(i, h):
+            nc.vector.tensor_tensor(out=out_sb[:, i, half(h)], in0=o_banks[i, h][:], in1=x_plus_b[:, i, half(h)], op=ALU.add)
+            nc.sync.dma_start(out=out_rows[:, i, half(h)], in_=out_sb[:, i, half(h)])
 
         k_copies = (nc.scalar.copy, nc.vector.tensor_copy)
         with tc.manual_schedule():
@@ -278,45 +287,67 @@ def tile_transformerblock_pa_kernel(tc, q, k, v, x, w_proj, b_proj, out):
             transpose_q(0, nc.vector.tensor_copy)
             for u in range(K_AHEAD):
                 transpose_k(u, k_copies[u % 2])
+            spread_b()
+            for u in range(K_AHEAD, WORD_CHUNKS):
+                transpose_k(u, k_copies[u % 2])
             for r in range(Q_TILES + 2):
+                if not live(r):
+                    spread_inv(r - 2)
                 for c in range(E_CHUNKS if live(r) else 0):
-                    if r == 0 and c % 2 == 0 and c // 2 + K_AHEAD < WORD_CHUNKS:
-                        transpose_k(c // 2 + K_AHEAD, nc.scalar.copy)
                     if (r, c) in Q_TURNS:
                         transpose_q(Q_TURNS.index((r, c)) + 1, nc.scalar.copy)
-                    if (r, c) == (0, 2):
-                        spread_b()
+                    if c == 2 and live(r - 2):
+                        spread_inv(r - 2)
+                    if (r, c) == (1, 5):
+                        copy_b()
                     score_matmul(r, c)
                 if r == 0:
                     regroup_v(0, nc.vector.tensor_copy, 0, BANK)
                     regroup_v(1, nc.scalar.copy, BANK // 2, BANK)
                     regroup_v(1, nc.vector.tensor_copy, 0, BANK // 2)
-                    quantise_v(0)
                 if live(r - 1):
                     transpose_e(r - 1)
-                    spread_inv(r - 1)
                 if live(r - 2):
                     attend(r - 2)
+                if r == 4:
+                    project(0, 0)
+                    project(1, 0)
+                if r == 5:
+                    project(2, 0)
                 if live(r):
                     softmax_max(r)
                     softmax_exp(r)
-                if live(r - 1):
-                    regroup_w(r - 1, nc.scalar.copy, V_SHARE, BANK)
+                for piece, part in S_PARTS.get(r, ()):
+                    regroup_w(piece, nc.scalar.copy, part * BANK // 2, (part + 1) * BANK // 2)
                 if r == 0:
+                    quantise_v(0)
                     quantise_v(1)
+                if r == 5:
+                    finish(0, 0)
                 if live(r - 2):
                     normalise(r - 2)
+                if r == 5:
+                    finish(1, 0)
                 if live(r - 1):
                     quantise_e(r - 1)
+                if r < HALVES:
+                    regroup_w(r, nc.vector.tensor_copy, 0, V_COLS[r])
                 if live(r):
-                    regroup_w(r, nc.vector.tensor_copy, 0, V_SHARE)
                     softmax_inv(r)
-                if live(r - 2):
+                if live(r - 2) and r < 5:
                     quantise_attn(r - 2)
-                if live(r - 2):
-                    quantise_w(r - 2)
-                if r == 2:
+                for piece in W_QUANT.get(r, ()):
+                    quantise_w(piece)
+                if r == 1:
                     for i in range(Q_TILES):
                         add_x_b(i)
-            for i in range(Q_TILES):
-                project(i)
+            quantise_attn(3)
+            finish(2, 0)
+            for i in range(Q_TILES - 1):
+                project(i, 1)
+            for h in range(HALVES):
+                project(3, h)
+            for i in range(Q_TILES - 1):
+                finish(i, 1)
+            for h in range(HALVES):
+                finish(3, h)

@@ -26,13 +26,12 @@ WORD_CHUNKS = E // (2 * P)
 F_PASSES = E // (P * PACK)
 HALVES = E // BANK
 WARM_UPS = 4
-Q_TURNS = ((0, 4), (1, 0), (1, 3))
-K_AHEAD = 2
+Q_TURNS = ((0, 0), (1, 2), (1, 4))
 XB_PIECE = 256
 
 S_PARTS = {1: ((2, 0),), 2: ((2, 1),), 3: ((3, 0),), 4: ((3, 1),)}
 V_COLS = (BANK, BANK)
-W_QUANT = {0: (0,), 1: (1,), 3: (2,), 5: (3,)}
+W_QUANT = {0: (0,), 1: (1,), 3: (2,)}
 
 FLOPS = 2 * S * S * E + 2 * S * S * E + 2 * S * E * E
 
@@ -43,22 +42,22 @@ def tile_transformerblock_pa_kernel(tc, q, k, v, x, w_proj, b_proj, out):
         keep = ctx.enter_context(tc.tile_pool(name="keep", bufs=1))
         psum = ctx.enter_context(tc.psum_pool(name="psum", bufs=8))
 
-        q_rows = q.flatten_outer_dims().rearrange("(i p) e -> p i e", p=P)
-        x_rows = x.flatten_outer_dims().rearrange("(i p) n -> p i n", p=P)
-        out_rows = out.flatten_outer_dims().rearrange("(i p) n -> p i n", p=P)
+        q_rows = q.flatten_outer_dims().rearrange("(p i) e -> p i e", p=P)
+        x_rows = x.flatten_outer_dims().rearrange("(p i) n -> p i n", p=P)
+        out_rows = out.flatten_outer_dims().rearrange("(p i) n -> p i n", p=P)
         k_rows = k.flatten_outer_dims().rearrange("(p t) e -> p t e", t=PACK)
         v_rows = v.flatten_outer_dims().rearrange("(p t) f -> p t f", t=PACK)
         w_rows = w_proj.rearrange("(g t p) n -> p g t n", t=PACK, p=P)
 
         q_raw = keep.tile([P, Q_TILES, E], BF16, name="q_raw")
-        k_raw = [keep.tile([P, PACK, BANK], BF16, name=f"k_raw{h}") for h in range(HALVES)]
+        k_raw = [keep.tile([P, PACK // HALVES, E], BF16, name=f"k_raw{h}") for h in range(HALVES)]
         v_raw = [keep.tile([P, PACK, BANK], BF16, name=f"v_raw{h}") for h in range(HALVES)]
         w_raw = [keep.tile([P, PACK, BANK], BF16, name=f"w_raw{r}") for r in range(HALVES * F_PASSES)]
         x_raw = keep.tile([P, Q_TILES, E], BF16, name="x_raw")
         b_rows = keep.tile([P, E], BF16, name="b_rows")
 
         qT = keep.tile([P, Q_TILES, WORD_CHUNKS, P, 2], BF16, name="qT")
-        kT = keep.tile([P, WORD_CHUNKS, S, 2], BF16, name="kT")
+        kT = keep.tile([P, HALVES, WORD_CHUNKS, S // HALVES, 2], BF16, name="kT")
 
         v_grouped = keep.tile([P, E, PACK], BF16, name="v_grouped", align_bytes=64)
         v_codes = keep.tile([P, E], U32, name="v_codes", align_bytes=64)
@@ -107,14 +106,14 @@ def tile_transformerblock_pa_kernel(tc, q, k, v, x, w_proj, b_proj, out):
 
         nc.sync.dma_start(out=q_raw[:, 0, :], in_=q_rows[:, 0, :])
         for h in range(HALVES):
-            nc.sync.dma_start(out=k_raw[h][:], in_=k_rows[:, :, half(h)])
+            nc.sync.dma_start(out=k_raw[h][:], in_=k_rows[:, h * PACK // HALVES : (h + 1) * PACK // HALVES, :])
             if h == 0:
                 nc.sync.dma_start(out=b_rows[0:1, :], in_=b_proj.rearrange("(o n) -> o n", o=1))
-        nc.sync.dma_start(out=q_raw[:, 1, :], in_=q_rows[:, 1, :])
         for h in range(HALVES):
             nc.sync.dma_start(out=v_raw[h][:], in_=v_rows[:, :, half(h)])
-        for i in range(2, Q_TILES):
-            nc.sync.dma_start(out=q_raw[:, i, :], in_=q_rows[:, i, :])
+            if h == 0:
+                nc.sync.dma_start(out=q_raw[:, 1, :], in_=q_rows[:, 1, :])
+        nc.sync.dma_start(out=q_raw[:, 2:, :], in_=q_rows[:, 2:, :])
         for h in range(HALVES):
             for g in range(F_PASSES):
                 nc.sync.dma_start(out=w_raw[h * F_PASSES + g][:], in_=w_rows[:, g, :, half(h)])
@@ -151,10 +150,11 @@ def tile_transformerblock_pa_kernel(tc, q, k, v, x, w_proj, b_proj, out):
             blocks = [words[:, u * P : (u + 1) * P] for u in range(WORD_CHUNKS)]
             transpose_words(blocks, qT[:, i].rearrange("p u r e -> p (u r e)").bitcast(F32), copy)
 
-        def transpose_k(u, copy):
-            h, first = u // HALVES, u % HALVES * P
-            blocks = [k_raw[h][:, t, :].bitcast(F32)[:, first : first + P] for t in range(PACK)]
-            transpose_words(blocks, kT[:, u].rearrange("p s e -> p (s e)").bitcast(F32), copy)
+        def transpose_k(h, pair, copy):
+            chunks = range(2 * pair, 2 * pair + 2)
+            words = [k_raw[h][:, t, :].bitcast(F32) for t in range(PACK // HALVES)]
+            blocks = [word[:, u * P : (u + 1) * P] for u in chunks for word in words]
+            transpose_words(blocks, kT[:, h, chunks.start : chunks.stop].rearrange("p u s e -> p (u s e)").bitcast(F32), copy)
 
         def regroup(copy, grouped, raw):
             copy(
@@ -189,13 +189,12 @@ def tile_transformerblock_pa_kernel(tc, q, k, v, x, w_proj, b_proj, out):
         b_banks = {}
         o_banks = {}
 
-        def score_matmul(i, c):
-            if c == 0:
-                s_banks[i] = psum.tile([P, S], F32, name="s_bank", tag="bank")
+        def score_matmul(i, c, keys):
+            s_bank = s_banks[i][:].rearrange("p (h s) -> p h s", h=HALVES)
             nc.tensor.matmul(
-                s_banks[i][:],
+                s_bank[:, keys, :],
                 lhsT=qT[:, i, c // 2, :, c % 2],
-                rhs=kT[:, c // 2, :, c % 2],
+                rhs=kT[:, keys, c // 2, :, c % 2],
                 start=(c == 0),
                 stop=(c == E_CHUNKS - 1),
             )
@@ -285,22 +284,26 @@ def tile_transformerblock_pa_kernel(tc, q, k, v, x, w_proj, b_proj, out):
         with tc.manual_schedule():
             warm_up()
             transpose_q(0, nc.vector.tensor_copy)
-            for u in range(K_AHEAD):
-                transpose_k(u, k_copies[u % 2])
+            for pair in range(2):
+                transpose_k(0, pair, k_copies[pair])
             spread_b()
-            for u in range(K_AHEAD, WORD_CHUNKS):
-                transpose_k(u, k_copies[u % 2])
+            for pair in range(2):
+                transpose_k(1, pair, k_copies[pair])
+            copy_b()
             for r in range(Q_TILES + 2):
                 if not live(r):
                     spread_inv(r - 2)
+                if live(r):
+                    s_banks[r] = psum.tile([P, S], F32, name="s_bank", tag="bank")
+                if r == 0:
+                    for c in range(E_CHUNKS):
+                        score_matmul(0, c, slice(0, 1))
                 for c in range(E_CHUNKS if live(r) else 0):
                     if (r, c) in Q_TURNS:
                         transpose_q(Q_TURNS.index((r, c)) + 1, nc.scalar.copy)
                     if c == 2 and live(r - 2):
                         spread_inv(r - 2)
-                    if (r, c) == (1, 5):
-                        copy_b()
-                    score_matmul(r, c)
+                    score_matmul(r, c, slice(1 if r == 0 else 0, HALVES))
                 if r == 0:
                     regroup_v(0, nc.vector.tensor_copy, 0, BANK)
                     regroup_v(1, nc.scalar.copy, BANK // 2, BANK)
@@ -323,6 +326,7 @@ def tile_transformerblock_pa_kernel(tc, q, k, v, x, w_proj, b_proj, out):
                     quantise_v(0)
                     quantise_v(1)
                 if r == 5:
+                    quantise_w(3)
                     finish(0, 0)
                 if live(r - 2):
                     normalise(r - 2)

@@ -25,13 +25,8 @@ E_CHUNKS = E // P
 WORD_CHUNKS = E // (2 * P)
 F_PASSES = E // (P * PACK)
 HALVES = E // BANK
-WARM_UPS = 4
-Q_TURNS = ((0, 0), (1, 2), (1, 4))
 XB_PIECE = 256
 
-S_PARTS = {1: ((2, 0),), 2: ((2, 1),), 3: ((3, 0),), 4: ((3, 1),)}
-V_COLS = (BANK, BANK)
-W_QUANT = {0: (0,), 1: (1,), 3: (2,)}
 
 FLOPS = 2 * S * S * E + 2 * S * S * E + 2 * S * E * E
 
@@ -105,20 +100,19 @@ def tile_transformerblock_pa_kernel(tc, q, k, v, x, w_proj, b_proj, out):
         nc.scalar.activation(out=table_warm[:], in_=ones_bf[:, 0:1], func=ACT.Exp)
 
         nc.sync.dma_start(out=q_raw[:, 0, :], in_=q_rows[:, 0, :])
-        for h in range(HALVES):
-            nc.sync.dma_start(out=k_raw[h][:], in_=k_rows[:, h * PACK // HALVES : (h + 1) * PACK // HALVES, :])
-            if h == 0:
-                nc.sync.dma_start(out=b_rows[0:1, :], in_=b_proj.rearrange("(o n) -> o n", o=1))
-        for h in range(HALVES):
-            nc.sync.dma_start(out=v_raw[h][:], in_=v_rows[:, :, half(h)])
-            if h == 0:
-                nc.sync.dma_start(out=q_raw[:, 1, :], in_=q_rows[:, 1, :])
+        nc.sync.dma_start(out=k_raw[0][:], in_=k_rows[:, 0 : 2, :])
+        nc.sync.dma_start(out=b_rows[0:1, :], in_=b_proj.rearrange("(o n) -> o n", o=1))
+        nc.sync.dma_start(out=k_raw[1][:], in_=k_rows[:, 2 : 4, :])
+        nc.sync.dma_start(out=v_raw[0][:], in_=v_rows[:, :, half(0)])
+        nc.sync.dma_start(out=q_raw[:, 1, :], in_=q_rows[:, 1, :])
+        nc.sync.dma_start(out=v_raw[1][:], in_=v_rows[:, :, half(1)])
         nc.sync.dma_start(out=q_raw[:, 2:, :], in_=q_rows[:, 2:, :])
-        for h in range(HALVES):
-            for g in range(F_PASSES):
-                nc.sync.dma_start(out=w_raw[h * F_PASSES + g][:], in_=w_rows[:, g, :, half(h)])
-            tiles = slice(h * Q_TILES // HALVES, (h + 1) * Q_TILES // HALVES)
-            nc.sync.dma_start(out=x_raw[:, tiles, :], in_=x_rows[:, tiles, :])
+        nc.sync.dma_start(out=w_raw[0][:], in_=w_rows[:, 0, :, half(0)])
+        nc.sync.dma_start(out=w_raw[1][:], in_=w_rows[:, 1, :, half(0)])
+        nc.sync.dma_start(out=x_raw[:, 0 : 2, :], in_=x_rows[:, 0 : 2, :])
+        nc.sync.dma_start(out=w_raw[2][:], in_=w_rows[:, 0, :, half(1)])
+        nc.sync.dma_start(out=w_raw[3][:], in_=w_rows[:, 1, :, half(1)])
+        nc.sync.dma_start(out=x_raw[:, 2 : 4, :], in_=x_rows[:, 2 : 4, :])
 
         def spread_b():
             for h in range(HALVES):
@@ -129,9 +123,9 @@ def tile_transformerblock_pa_kernel(tc, q, k, v, x, w_proj, b_proj, out):
             for h in range(HALVES):
                 nc.scalar.copy(out=b_spread[:, half(h)], in_=b_banks[h][:])
 
-        def warm_up():
+        def warm_up(count):
             bank = psum.tile([P, BANK], F32, name="warm_bank", tag="bank")
-            for n in range(WARM_UPS):
+            for n in range(count):
                 nc.tensor.matmul(bank[:], lhsT=warm[:, 0:P], rhs=warm[:], start=True, stop=True)
 
         def add_x_b(i):
@@ -280,78 +274,107 @@ def tile_transformerblock_pa_kernel(tc, q, k, v, x, w_proj, b_proj, out):
             nc.vector.tensor_tensor(out=out_sb[:, i, half(h)], in0=o_banks[i, h][:], in1=x_plus_b[:, i, half(h)], op=ALU.add)
             nc.sync.dma_start(out=out_rows[:, i, half(h)], in_=out_sb[:, i, half(h)])
 
-        k_copies = (nc.scalar.copy, nc.vector.tensor_copy)
         with tc.manual_schedule():
-            warm_up()
+            warm_up(2)
             transpose_q(0, nc.vector.tensor_copy)
-            for pair in range(2):
-                transpose_k(0, pair, k_copies[pair])
+            warm_up(2)
+            transpose_k(0, 0, nc.scalar.copy)
+            transpose_k(0, 1, nc.vector.tensor_copy)
             spread_b()
-            for pair in range(2):
-                transpose_k(1, pair, k_copies[pair])
+            transpose_k(1, 1, nc.vector.tensor_copy)
+            transpose_k(1, 0, nc.scalar.copy)
             copy_b()
-            for r in range(Q_TILES + 2):
-                if not live(r):
-                    spread_inv(r - 2)
-                if live(r):
-                    s_banks[r] = psum.tile([P, S], F32, name="s_bank", tag="bank")
-                if r == 0:
-                    for c in range(E_CHUNKS):
-                        score_matmul(0, c, slice(0, 1))
-                for c in range(E_CHUNKS if live(r) else 0):
-                    if (r, c) in Q_TURNS:
-                        transpose_q(Q_TURNS.index((r, c)) + 1, nc.scalar.copy)
-                    if c == 2 and live(r - 2):
-                        spread_inv(r - 2)
-                    score_matmul(r, c, slice(1 if r == 0 else 0, HALVES))
-                if r == 0:
-                    regroup_v(0, nc.vector.tensor_copy, 0, BANK)
-                    regroup_v(1, nc.scalar.copy, BANK // 2, BANK)
-                    regroup_v(1, nc.vector.tensor_copy, 0, BANK // 2)
-                if live(r - 1):
-                    transpose_e(r - 1)
-                if live(r - 2):
-                    attend(r - 2)
-                if r == 4:
-                    project(0, 0)
-                    project(1, 0)
-                if r == 5:
-                    project(2, 0)
-                if live(r):
-                    softmax_max(r)
-                    softmax_exp(r)
-                for piece, part in S_PARTS.get(r, ()):
-                    regroup_w(piece, nc.scalar.copy, part * BANK // 2, (part + 1) * BANK // 2)
-                if r == 0:
-                    quantise_v(0)
-                    quantise_v(1)
-                if r == 5:
-                    quantise_w(3)
-                    finish(0, 0)
-                if live(r - 2):
-                    normalise(r - 2)
-                if r == 5:
-                    finish(1, 0)
-                if live(r - 1):
-                    quantise_e(r - 1)
-                if r < HALVES:
-                    regroup_w(r, nc.vector.tensor_copy, 0, V_COLS[r])
-                if live(r):
-                    softmax_inv(r)
-                if live(r - 2) and r < 5:
-                    quantise_attn(r - 2)
-                for piece in W_QUANT.get(r, ()):
-                    quantise_w(piece)
-                if r == 1:
-                    for i in range(Q_TILES):
-                        add_x_b(i)
-            quantise_attn(3)
+            s_banks[0] = psum.tile([P, S], F32, name="s_bank", tag="bank")
+            for c in range(E_CHUNKS):
+                score_matmul(0, c, slice(0, 1))
+            transpose_q(1, nc.scalar.copy)
+            for c in range(0, 8):
+                score_matmul(0, c, slice(1, HALVES))
+            regroup_v(0, nc.vector.tensor_copy, 0, 512)
+            regroup_v(1, nc.scalar.copy, 256, 512)
+            quantise_v(0)
+            regroup_v(1, nc.vector.tensor_copy, 0, 256)
+            softmax_max(0)
+            softmax_exp(0)
+            quantise_v(1)
+            regroup_w(0, nc.vector.tensor_copy, 0, 512)
+            softmax_inv(0)
+            quantise_w(0)
+            s_banks[1] = psum.tile([P, S], F32, name="s_bank", tag="bank")
+            for c in range(0, 2):
+                score_matmul(1, c, slice(0, HALVES))
+            transpose_q(2, nc.scalar.copy)
+            for c in range(2, 8):
+                score_matmul(1, c, slice(0, HALVES))
+            transpose_e(0)
+            transpose_q(3, nc.scalar.copy)
+            softmax_max(1)
+            softmax_exp(1)
+            regroup_w(2, nc.scalar.copy, 0, 256)
+            quantise_e(0)
+            regroup_w(1, nc.vector.tensor_copy, 0, 512)
+            softmax_inv(1)
+            quantise_w(1)
+            add_x_b(0)
+            add_x_b(1)
+            add_x_b(2)
+            add_x_b(3)
+            s_banks[2] = psum.tile([P, S], F32, name="s_bank", tag="bank")
+            for c in range(0, 2):
+                score_matmul(2, c, slice(0, HALVES))
+            spread_inv(0)
+            for c in range(2, 8):
+                score_matmul(2, c, slice(0, HALVES))
+            transpose_e(1)
+            attend(0)
+            softmax_max(2)
+            softmax_exp(2)
+            regroup_w(2, nc.scalar.copy, 256, 512)
+            normalise(0)
+            quantise_e(1)
+            softmax_inv(2)
+            quantise_attn(0)
+            s_banks[3] = psum.tile([P, S], F32, name="s_bank", tag="bank")
+            for c in range(0, 2):
+                score_matmul(3, c, slice(0, HALVES))
+            spread_inv(1)
+            for c in range(2, 8):
+                score_matmul(3, c, slice(0, HALVES))
+            transpose_e(2)
+            attend(1)
+            softmax_max(3)
+            softmax_exp(3)
+            regroup_w(3, nc.scalar.copy, 0, 256)
+            normalise(1)
+            quantise_e(2)
+            softmax_inv(3)
+            quantise_w(2)
+            quantise_attn(1)
+            spread_inv(2)
+            project(0, 0)
+            transpose_e(3)
+            attend(2)
+            project(1, 0)
+            regroup_w(3, nc.scalar.copy, 256, 512)
+            normalise(2)
+            quantise_e(3)
+            quantise_attn(2)
+            spread_inv(3)
+            attend(3)
+            project(2, 0)
+            quantise_w(3)
+            finish(0, 0)
+            normalise(3)
+            finish(1, 0)
             finish(2, 0)
-            for i in range(Q_TILES - 1):
-                project(i, 1)
-            for h in range(HALVES):
-                project(3, h)
-            for i in range(Q_TILES - 1):
-                finish(i, 1)
-            for h in range(HALVES):
-                finish(3, h)
+            quantise_attn(3)
+            project(0, 1)
+            project(1, 1)
+            project(2, 1)
+            project(3, 0)
+            project(3, 1)
+            finish(0, 1)
+            finish(1, 1)
+            finish(2, 1)
+            finish(3, 0)
+            finish(3, 1)

@@ -296,25 +296,23 @@ def tile_transformerblock_pa_kernel(tc, q, k, v, x, w_proj, b_proj, out):
             regroup_v(1, nc.vector.tensor_copy, 0, 256)
             softmax_max(0)
             softmax_exp(0)
+            softmax_inv(0)
             quantise_v(1)
             regroup_w(0, nc.vector.tensor_copy, 0, 512)
-            softmax_inv(0)
-            quantise_w(0)
             s_banks[1] = psum.tile([P, S], F32, name="s_bank", tag="bank")
-            for c in range(0, 2):
+            for c in range(0, 4):
                 score_matmul(1, c, slice(0, HALVES))
             transpose_q(2, nc.scalar.copy)
-            for c in range(2, 8):
+            for c in range(4, 8):
                 score_matmul(1, c, slice(0, HALVES))
             transpose_e(0)
             transpose_q(3, nc.scalar.copy)
             softmax_max(1)
             softmax_exp(1)
-            regroup_w(2, nc.scalar.copy, 0, 256)
+            quantise_w(0)
             quantise_e(0)
             regroup_w(1, nc.vector.tensor_copy, 0, 512)
             softmax_inv(1)
-            quantise_w(1)
             add_x_b(0)
             add_x_b(1)
             add_x_b(2)
@@ -329,9 +327,10 @@ def tile_transformerblock_pa_kernel(tc, q, k, v, x, w_proj, b_proj, out):
             attend(0)
             softmax_max(2)
             softmax_exp(2)
-            regroup_w(2, nc.scalar.copy, 256, 512)
+            regroup_w(2, nc.scalar.copy, 0, 256)
             normalise(0)
             quantise_e(1)
+            quantise_w(1)
             softmax_inv(2)
             quantise_attn(0)
             s_banks[3] = psum.tile([P, S], F32, name="s_bank", tag="bank")
@@ -344,27 +343,28 @@ def tile_transformerblock_pa_kernel(tc, q, k, v, x, w_proj, b_proj, out):
             attend(1)
             softmax_max(3)
             softmax_exp(3)
-            regroup_w(3, nc.scalar.copy, 0, 256)
             normalise(1)
             quantise_e(2)
             softmax_inv(3)
-            quantise_w(2)
             quantise_attn(1)
             spread_inv(2)
             project(0, 0)
             transpose_e(3)
             attend(2)
+            regroup_w(2, nc.scalar.copy, 256, 512)
             project(1, 0)
-            regroup_w(3, nc.scalar.copy, 256, 512)
+            regroup_w(3, nc.scalar.copy, 0, 256)
             normalise(2)
             quantise_e(3)
+            quantise_w(2)
             quantise_attn(2)
             spread_inv(3)
+            regroup_w(3, nc.scalar.copy, 256, 512)
             attend(3)
             project(2, 0)
-            quantise_w(3)
             finish(0, 0)
             normalise(3)
+            quantise_w(3)
             finish(1, 0)
             finish(2, 0)
             quantise_attn(3)

@@ -25,7 +25,6 @@ E_CHUNKS = E // P
 WORD_CHUNKS = E // (2 * P)
 F_PASSES = E // (P * PACK)
 HALVES = E // BANK
-XB_PIECE = 256
 
 
 FLOPS = 2 * S * S * E + 2 * S * S * E + 2 * S * E * E
@@ -128,10 +127,14 @@ def tile_transformerblock_pa_kernel(tc, q, k, v, x, w_proj, b_proj, out):
             for n in range(count):
                 nc.tensor.matmul(bank[:], lhsT=warm[:, 0:P], rhs=warm[:], start=True, stop=True)
 
-        def add_x_b(i):
-            for j in range(E // XB_PIECE):
-                cols = slice(j * XB_PIECE, (j + 1) * XB_PIECE)
-                nc.gpsimd.tensor_tensor(out=x_plus_b[:, i, cols], in0=x_raw[:, i, cols], in1=b_spread[:, cols], op=ALU.add)
+        def add_x_b(halves, i, width):
+            for h in halves:
+                for j in range(BANK // width):
+                    cols = slice(h * BANK + j * width, h * BANK + (j + 1) * width)
+                    nc.gpsimd.tensor_tensor(out=x_plus_b[:, i, cols], in0=x_raw[:, i, cols], in1=b_spread[:, cols], op=ALU.add)
+
+        def add_x_b_by_vector(i, h):
+            nc.vector.tensor_tensor(out=x_plus_b[:, i, half(h)], in0=b_banks[h][:], in1=x_raw[:, i, half(h)], op=ALU.add)
 
         def transpose_words(blocks, dst, copy):
             bank = psum.tile([P, PACK, P], F32, name="t_bank", tag="bank")
@@ -296,8 +299,8 @@ def tile_transformerblock_pa_kernel(tc, q, k, v, x, w_proj, b_proj, out):
             regroup_v(1, nc.vector.tensor_copy, 0, 256)
             softmax_max(0)
             softmax_exp(0)
-            softmax_inv(0)
             quantise_v(1)
+            softmax_inv(0)
             regroup_w(0, nc.vector.tensor_copy, 0, 512)
             s_banks[1] = psum.tile([P, S], F32, name="s_bank", tag="bank")
             for c in range(0, 4):
@@ -313,10 +316,10 @@ def tile_transformerblock_pa_kernel(tc, q, k, v, x, w_proj, b_proj, out):
             quantise_e(0)
             regroup_w(1, nc.vector.tensor_copy, 0, 512)
             softmax_inv(1)
-            add_x_b(0)
-            add_x_b(1)
-            add_x_b(2)
-            add_x_b(3)
+            add_x_b(range(HALVES), 0, 256)
+            add_x_b(range(HALVES), 1, 256)
+            add_x_b(range(HALVES), 2, 256)
+            add_x_b((0,), 3, 256)
             s_banks[2] = psum.tile([P, S], F32, name="s_bank", tag="bank")
             for c in range(0, 2):
                 score_matmul(2, c, slice(0, HALVES))
@@ -348,12 +351,13 @@ def tile_transformerblock_pa_kernel(tc, q, k, v, x, w_proj, b_proj, out):
             softmax_inv(3)
             quantise_attn(1)
             spread_inv(2)
-            project(0, 0)
             transpose_e(3)
             attend(2)
+            project(0, 0)
             regroup_w(2, nc.scalar.copy, 256, 512)
             project(1, 0)
             regroup_w(3, nc.scalar.copy, 0, 256)
+            add_x_b_by_vector(3, 1)
             normalise(2)
             quantise_e(3)
             quantise_w(2)
@@ -362,9 +366,9 @@ def tile_transformerblock_pa_kernel(tc, q, k, v, x, w_proj, b_proj, out):
             regroup_w(3, nc.scalar.copy, 256, 512)
             attend(3)
             project(2, 0)
-            finish(0, 0)
             normalise(3)
             quantise_w(3)
+            finish(0, 0)
             finish(1, 0)
             finish(2, 0)
             quantise_attn(3)

from contextlib import ExitStack

import concourse.mybir as mybir
from concourse.masks import make_identity

F32 = mybir.dt.float32
BF16 = mybir.dt.bfloat16
U32 = mybir.dt.uint32
U8 = mybir.dt.uint8
FP8X4 = mybir.dt.float8_e4m3fn_x4
ALU = mybir.AluOpType
ACT = mybir.ActivationFunctionType
AXIS = mybir.AxisListType

P = 128
PACK = 4
S = 512
E = 1024
HEAD = 64
BANK = 512
SCORE_SCALE = HEAD**-0.5

Q_TILES = S // P
E_CHUNKS = E // P
WORD_CHUNKS = E // (2 * P)
F_PASSES = E // (P * PACK)
HALVES = E // BANK


FLOPS = 2 * S * S * E + 2 * S * S * E + 2 * S * E * E


def tile_transformerblock_pa_kernel(tc, q, k, v, x, w_proj, b_proj, out):
    nc = tc.nc
    with ExitStack() as ctx:
        keep = ctx.enter_context(tc.tile_pool(name="keep", bufs=1))
        psum = ctx.enter_context(tc.psum_pool(name="psum", bufs=8))

        q_rows = q.flatten_outer_dims().rearrange("(p i) e -> p i e", p=P)
        x_rows = x.flatten_outer_dims().rearrange("(p i) n -> p i n", p=P)
        out_rows = out.flatten_outer_dims().rearrange("(p i) n -> p i n", p=P)
        k_rows = k.flatten_outer_dims().rearrange("(p t) e -> p t e", t=PACK)
        v_rows = v.flatten_outer_dims().rearrange("(p t) f -> p t f", t=PACK)
        w_rows = w_proj.rearrange("(g t p) n -> p g t n", t=PACK, p=P)

        q_raw = keep.tile([P, Q_TILES, E], BF16, name="q_raw")
        k_raw = [keep.tile([P, PACK // HALVES, E], BF16, name=f"k_raw{h}") for h in range(HALVES)]
        v_raw = [keep.tile([P, PACK, BANK], BF16, name=f"v_raw{h}") for h in range(HALVES)]
        w_raw = [keep.tile([P, PACK, BANK], BF16, name=f"w_raw{r}") for r in range(HALVES * F_PASSES)]
        x_raw = keep.tile([P, Q_TILES, E], BF16, name="x_raw")
        b_rows = keep.tile([P, E], BF16, name="b_rows")

        qT = keep.tile([P, Q_TILES, WORD_CHUNKS, P, 2], BF16, name="qT")
        kT = keep.tile([P, HALVES, WORD_CHUNKS, S // HALVES, 2], BF16, name="kT")

        v_grouped = keep.tile([P, E, PACK], BF16, name="v_grouped", align_bytes=64)
        v_codes = keep.tile([P, E], U32, name="v_codes", align_bytes=64)
        v_scales = keep.tile([P, E], U8, name="v_scales", align_bytes=64)
        w_grouped = keep.tile([P, F_PASSES, E, PACK], BF16, name="w_grouped", align_bytes=64)
        w_codes = keep.tile([P, F_PASSES, E], U32, name="w_codes", align_bytes=64)
        w_scales = keep.tile([P, F_PASSES, E], U8, name="w_scales", align_bytes=64)

        e_bf = keep.tile([P, Q_TILES, S], BF16, name="e_bf")
        e_grouped = keep.tile([P, Q_TILES, P, PACK], BF16, name="e_grouped", align_bytes=64)
        e_codes = keep.tile([P, Q_TILES, P], U32, name="e_codes", align_bytes=64)
        e_scales = keep.tile([P, Q_TILES, P], U8, name="e_scales", align_bytes=64)

        attn_grouped = keep.tile([P, Q_TILES, F_PASSES, P, PACK], BF16, name="attn_grouped", align_bytes=64)
        attn_codes = keep.tile([P, Q_TILES, F_PASSES, P], U32, name="attn_codes", align_bytes=64)
        attn_scales = keep.tile([P, Q_TILES, F_PASSES, P], U8, name="attn_scales", align_bytes=64)

        row_max = keep.tile([P, Q_TILES], F32, name="row_max")
        exp_bias = keep.tile([P, Q_TILES], F32, name="exp_bias")
        row_sum = keep.tile([P, Q_TILES], F32, name="row_sum")
        row_inv = keep.tile([P, Q_TILES], F32, name="row_inv")
        inv_spread = keep.tile([P, Q_TILES, P], F32, name="inv_spread")

        b_spread = keep.tile([P, E], BF16, name="b_spread")
        x_plus_b = keep.tile([P, Q_TILES, E], F32, name="x_plus_b")
        out_sb = keep.tile([P, Q_TILES, E], F32, name="out_sb")

        ident_bf = keep.tile([P, P], BF16, name="ident_bf")
        ident_f32 = keep.tile([P, P], F32, name="ident_f32")
        ones_bf = keep.tile([P, P], BF16, name="ones_bf")
        warm = keep.tile([P, BANK], BF16, name="warm")
        table_warm = keep.tile([P, 1], F32, name="table_warm")

        def half(h):
            return slice(h * BANK, (h + 1) * BANK)

        def live(i):
            return 0 <= i < Q_TILES

        make_identity(nc, ident_f32[:])
        make_identity(nc, ident_bf[:])
        nc.vector.memset(warm[:].bitcast(U32), 0)
        nc.vector.memset(b_rows[:].bitcast(U32), 0)
        nc.vector.memset(ones_bf[:], 1.0)
        nc.scalar.activation(out=table_warm[:], in_=ones_bf[:, 0:1], func=ACT.Exp)

        nc.sync.dma_start(out=q_raw[:, 0, :], in_=q_rows[:, 0, :])
        nc.sync.dma_start(out=k_raw[0][:], in_=k_rows[:, 0 : 2, :])
        nc.sync.dma_start(out=b_rows[0:1, :], in_=b_proj.rearrange("(o n) -> o n", o=1))
        nc.sync.dma_start(out=k_raw[1][:], in_=k_rows[:, 2 : 4, :])
        nc.sync.dma_start(out=v_raw[0][:], in_=v_rows[:, :, half(0)])
        nc.sync.dma_start(out=q_raw[:, 1, :], in_=q_rows[:, 1, :])
        nc.sync.dma_start(out=v_raw[1][:], in_=v_rows[:, :, half(1)])
        nc.sync.dma_start(out=q_raw[:, 2:, :], in_=q_rows[:, 2:, :])
        nc.sync.dma_start(out=w_raw[0][:], in_=w_rows[:, 0, :, half(0)])
        nc.sync.dma_start(out=w_raw[1][:], in_=w_rows[:, 1, :, half(0)])
        nc.sync.dma_start(out=x_raw[:, 0 : 2, :], in_=x_rows[:, 0 : 2, :])
        nc.sync.dma_start(out=w_raw[2][:], in_=w_rows[:, 0, :, half(1)])
        nc.sync.dma_start(out=w_raw[3][:], in_=w_rows[:, 1, :, half(1)])
        nc.sync.dma_start(out=x_raw[:, 2 : 4, :], in_=x_rows[:, 2 : 4, :])

        def spread_b():
            for h in range(HALVES):
                b_banks[h] = psum.tile([P, BANK], F32, name="b_bank", tag="bank")
                nc.tensor.matmul(b_banks[h][:], lhsT=ones_bf[:], rhs=b_rows[:, half(h)], start=True, stop=True)

        def copy_b():
            for h in range(HALVES):
                nc.scalar.copy(out=b_spread[:, half(h)], in_=b_banks[h][:])

        def warm_up(count):
            bank = psum.tile([P, BANK], F32, name="warm_bank", tag="bank")
            for n in range(count):
                nc.tensor.matmul(bank[:], lhsT=warm[:, 0:P], rhs=warm[:], start=True, stop=True)

        def add_x_b(halves, i, width):
            for h in halves:
                for j in range(BANK // width):
                    cols = slice(h * BANK + j * width, h * BANK + (j + 1) * width)
                    nc.gpsimd.tensor_tensor(out=x_plus_b[:, i, cols], in0=x_raw[:, i, cols], in1=b_spread[:, cols], op=ALU.add)

        def add_x_b_by_vector(i, h):
            nc.vector.tensor_tensor(out=x_plus_b[:, i, half(h)], in0=b_banks[h][:], in1=x_raw[:, i, half(h)], op=ALU.add)

        def transpose_words(blocks, dst, copy):
            bank = psum.tile([P, PACK, P], F32, name="t_bank", tag="bank")
            for j in range(PACK):
                nc.tensor.transpose(bank[:, j, :], blocks[j], ident_f32[:])
            copy(out=dst, in_=bank[:].rearrange("p j r -> p (j r)"))

        def transpose_q(i, copy):
            words = q_raw[:, i, :].bitcast(F32)
            blocks = [words[:, u * P : (u + 1) * P] for u in range(WORD_CHUNKS)]
            transpose_words(blocks, qT[:, i].rearrange("p u r e -> p (u r e)").bitcast(F32), copy)

        def transpose_k(h, pair, copy):
            chunks = range(2 * pair, 2 * pair + 2)
            words = [k_raw[h][:, t, :].bitcast(F32) for t in range(PACK // HALVES)]
            blocks = [word[:, u * P : (u + 1) * P] for u in chunks for word in words]
            transpose_words(blocks, kT[:, h, chunks.start : chunks.stop].rearrange("p u s e -> p (u s e)").bitcast(F32), copy)

        def regroup(copy, grouped, raw):
            copy(
                out=grouped.rearrange("p (c i) t -> p c t i", i=4),
                in_=raw.rearrange("p t (c i) -> p c t i", i=4),
            )

        def quantise(codes, scales, grouped):
            nc.vector.quantize_mx(out=codes.bitcast(FP8X4), scales=scales, in_=grouped)

        def regroup_v(h, copy, first, end):
            regroup(copy, v_grouped[:, h * BANK + first : h * BANK + end, :], v_raw[h][:, :, first:end])

        def quantise_v(h):
            quantise(v_codes[:, half(h)], v_scales[:, half(h)], v_grouped[:, half(h), :].rearrange("p c t -> p (c t)"))

        def w_piece(r):
            return r // F_PASSES, r % F_PASSES

        def regroup_w(r, copy, first, end):
            h, g = w_piece(r)
            regroup(copy, w_grouped[:, g, h * BANK + first : h * BANK + end, :], w_raw[r][:, :, first:end])

        def quantise_w(r):
            h, g = w_piece(r)
            quantise(
                w_codes[:, g, half(h)], w_scales[:, g, half(h)], w_grouped[:, g, half(h), :].rearrange("p c t -> p (c t)")
            )

        s_banks = {}
        a_banks = {}
        b_banks = {}
        o_banks = {}

        def score_matmul(i, c, keys):
            s_bank = s_banks[i][:].rearrange("p (h s) -> p h s", h=HALVES)
            nc.tensor.matmul(
                s_bank[:, keys, :],
                lhsT=qT[:, i, c // 2, :, c % 2],
                rhs=kT[:, keys, c // 2, :, c % 2],
                start=(c == 0),
                stop=(c == E_CHUNKS - 1),
            )

        def softmax_max(i):
            nc.vector.reduce_max(out=row_max[:, i : i + 1], in_=s_banks[i][:], axis=AXIS.X)

        def softmax_exp(i):
            one = slice(i, i + 1)
            nc.scalar.mul(out=exp_bias[:, one], in_=row_max[:, one], mul=-SCORE_SCALE)
            nc.scalar.activation(
                out=e_bf[:, i, :],
                in_=s_banks[i][:],
                func=ACT.Exp,
                bias=exp_bias[:, one],
                scale=SCORE_SCALE,
                accum_out=row_sum[:, one],
            )

        def softmax_inv(i):
            one = slice(i, i + 1)
            nc.vector.reciprocal(out=row_inv[:, one], in_=row_sum[:, one])

        def transpose_e(i):
            bank = psum.tile([P, PACK, P], BF16, name="e_bank", tag="bank")
            for t in range(PACK):
                nc.tensor.transpose(bank[:, t, :], e_bf[:, i, t * P : (t + 1) * P], ident_bf[:])
            nc.scalar.copy(out=e_grouped[:, i, :, :], in_=bank[:].rearrange("p t r -> p r t"))

        def quantise_e(i):
            quantise(e_codes[:, i, :], e_scales[:, i, :], e_grouped[:, i, :, :].rearrange("p r t -> p (r t)"))

        def spread_inv(i):
            inv_bank = psum.tile([P, P], F32, name="inv_bank", tag="bank")
            nc.tensor.transpose(inv_bank[:], row_inv[:, i : i + 1].to_broadcast([P, P]), ident_f32[:])
            nc.scalar.copy(out=inv_spread[:, i, :], in_=inv_bank[:])

        def attend(i):
            for g in range(F_PASSES):
                a_banks[i, g] = psum.tile([P, PACK, P], F32, name="a_bank", tag="bank")
                for t in range(PACK):
                    f_cols = slice((g * PACK + t) * P, (g * PACK + t + 1) * P)
                    nc.tensor.matmul_mx(
                        out=a_banks[i, g][:, t, :],
                        lhsT=v_codes[:, f_cols].bitcast(FP8X4),
                        lhsT_scale=v_scales[:, f_cols],
                        rhs=e_codes[:, i, :].bitcast(FP8X4),
                        rhs_scale=e_scales[:, i, :],
                        start=True,
                        stop=True,
                    )

        def normalise(i):
            for g in range(F_PASSES):
                nc.vector.tensor_tensor(
                    out=attn_grouped[:, i, g, :, :],
                    in0=a_banks[i, g][:].rearrange("p t r -> p r t"),
                    in1=inv_spread[:, i, :].unsqueeze(2).to_broadcast([P, P, PACK]),
                    op=ALU.mult,
                )

        def quantise_attn(i):
            quantise(
                attn_codes[:, i, :, :].rearrange("p g r -> p (g r)"),
                attn_scales[:, i, :, :].rearrange("p g r -> p (g r)"),
                attn_grouped[:, i, :, :, :].rearrange("p g r t -> p (g r t)"),
            )

        def project(i, h):
            o_bank = o_banks[i, h] = psum.tile([P, BANK], F32, name="o_bank", tag="bank")
            for g in range(F_PASSES):
                nc.tensor.matmul_mx(
                    out=o_bank[:],
                    lhsT=attn_codes[:, i, g, :].bitcast(FP8X4),
                    lhsT_scale=attn_scales[:, i, g, :],
                    rhs=w_codes[:, g, half(h)].bitcast(FP8X4),
                    rhs_scale=w_scales[:, g, half(h)],
                    start=(g == 0),
                    stop=(g == F_PASSES - 1),
                )

        def finish(i, h):
            nc.vector.tensor_tensor(out=out_sb[:, i, half(h)], in0=o_banks[i, h][:], in1=x_plus_b[:, i, half(h)], op=ALU.add)
            nc.sync.dma_start(out=out_rows[:, i, half(h)], in_=out_sb[:, i, half(h)])

        with tc.manual_schedule():
            warm_up(2)
            transpose_q(0, nc.vector.tensor_copy)
            warm_up(2)
            transpose_k(0, 0, nc.scalar.copy)
            transpose_k(0, 1, nc.vector.tensor_copy)
            spread_b()
            transpose_k(1, 1, nc.vector.tensor_copy)
            transpose_k(1, 0, nc.scalar.copy)
            copy_b()
            s_banks[0] = psum.tile([P, S], F32, name="s_bank", tag="bank")
            for c in range(E_CHUNKS):
                score_matmul(0, c, slice(0, 1))
            transpose_q(1, nc.scalar.copy)
            for c in range(0, 8):
                score_matmul(0, c, slice(1, HALVES))
            regroup_v(0, nc.vector.tensor_copy, 0, 512)
            regroup_v(1, nc.scalar.copy, 256, 512)
            quantise_v(0)
            regroup_v(1, nc.vector.tensor_copy, 0, 256)
            softmax_max(0)
            softmax_exp(0)
            quantise_v(1)
            softmax_inv(0)
            regroup_w(0, nc.vector.tensor_copy, 0, 512)
            s_banks[1] = psum.tile([P, S], F32, name="s_bank", tag="bank")
            for c in range(0, 4):
                score_matmul(1, c, slice(0, HALVES))
            transpose_q(2, nc.scalar.copy)
            for c in range(4, 8):
                score_matmul(1, c, slice(0, HALVES))
            transpose_e(0)
            transpose_q(3, nc.scalar.copy)
            softmax_max(1)
            softmax_exp(1)
            quantise_w(0)
            quantise_e(0)
            regroup_w(1, nc.vector.tensor_copy, 0, 512)
            softmax_inv(1)
            add_x_b(range(HALVES), 0, 256)
            add_x_b(range(HALVES), 1, 256)
            add_x_b(range(HALVES), 2, 256)
            add_x_b((0,), 3, 256)
            s_banks[2] = psum.tile([P, S], F32, name="s_bank", tag="bank")
            for c in range(0, 2):
                score_matmul(2, c, slice(0, HALVES))
            spread_inv(0)
            for c in range(2, 8):
                score_matmul(2, c, slice(0, HALVES))
            transpose_e(1)
            attend(0)
            softmax_max(2)
            softmax_exp(2)
            regroup_w(2, nc.scalar.copy, 0, 256)
            normalise(0)
            quantise_e(1)
            quantise_w(1)
            softmax_inv(2)
            quantise_attn(0)
            s_banks[3] = psum.tile([P, S], F32, name="s_bank", tag="bank")
            for c in range(0, 2):
                score_matmul(3, c, slice(0, HALVES))
            spread_inv(1)
            for c in range(2, 8):
                score_matmul(3, c, slice(0, HALVES))
            transpose_e(2)
            attend(1)
            softmax_max(3)
            softmax_exp(3)
            normalise(1)
            quantise_e(2)
            softmax_inv(3)
            quantise_attn(1)
            spread_inv(2)
            transpose_e(3)
            attend(2)
            project(0, 0)
            regroup_w(2, nc.scalar.copy, 256, 512)
            project(1, 0)
            regroup_w(3, nc.scalar.copy, 0, 256)
            add_x_b_by_vector(3, 1)
            normalise(2)
            quantise_e(3)
            quantise_w(2)
            quantise_attn(2)
            spread_inv(3)
            regroup_w(3, nc.scalar.copy, 256, 512)
            attend(3)
            project(2, 0)
            normalise(3)
            quantise_w(3)
            finish(0, 0)
            finish(1, 0)
            finish(2, 0)
            quantise_attn(3)
            project(0, 1)
            project(1, 1)
            project(2, 1)
            project(3, 0)
            project(3, 1)
            finish(0, 1)
            finish(1, 1)
            finish(2, 1)
            finish(3, 0)
            finish(3, 1)
